import numpy as np
import ml_dtypes


def mxq(x, axis, fmt="e4m3"):
    dtype, down = {"e4m3": (ml_dtypes.float8_e4m3fn, 7), "e5m2": (ml_dtypes.float8_e5m2, 14)}[fmt]
    v = np.moveaxis(np.asarray(x, np.float32).astype(ml_dtypes.bfloat16).astype(np.float64), axis, -1)
    blocks = v.reshape(v.shape[:-1] + (-1, 32))
    amax = np.abs(blocks).max(-1, keepdims=True)
    byte = np.maximum(np.where(amax > 0, np.frexp(amax)[1] - 1 + 127, 0) - down, 1)
    scale = np.exp2(byte - 127.0)
    codes = (blocks / scale).astype(np.float32).astype(dtype).astype(np.float64)
    return np.moveaxis((codes * scale).reshape(v.shape), -1, axis)


WIDE = False


def mx_kscale(k):
    if not WIDE:
        return np.ones(k)
    levels = np.array([10, -10, 5, -5, 0])
    a = np.random.permutation(np.resize(levels, k // 512 * 4)).reshape(k // 512, 4)
    idx = np.arange(k)
    return np.exp2(a[idx // 512, idx % 128 // 32])


BF16 = ml_dtypes.bfloat16


def bf(x):
    return np.asarray(x, np.float32).astype(BF16)


def f64(x):
    return np.asarray(x).astype(np.float64)


B, C, H, W, BH, BW, M = 4, 64, 35, 35, 4, 4, 1024
EPS = 1.0
N = C * BH * BW
HO, WO = H - BH + 1, W - BW + 1


def extract_patches(x):
    cols = [x[:, :, dh:dh + HO, dw:dw + WO] for dh in range(BH) for dw in range(BW)]
    return np.stack(cols, axis=2).reshape(B, N, HO, WO)


def setup_inputs():
    a = np.log(mx_kscale(N)[::BH * BW])
    return {"x": bf(np.random.standard_normal((B, C, H, W)) * 2.0 + a[None, :, None, None]),
            "offsets": bf(np.random.standard_normal((1, M, C, BH, BW)) * 2.0 - a[None, None, :, None, None])}


def reference(x, offsets):
    patches = extract_patches(f64(x))
    b = f64(offsets).reshape(M, N)
    m_x = np.max(EPS * patches, axis=1, keepdims=True)
    m_b = np.max(EPS * b, axis=1)
    Ex = np.exp(EPS * patches - m_x)
    Eb = np.exp(EPS * b - m_b[:, None])
    S = (mxq(Eb, 1, "e4m3") @ mxq(Ex.reshape(B, N, HO * WO), 1, "e4m3")).reshape(B, M, HO, WO)
    out = (m_x + m_b[None, :, None, None] + np.log(S)) / EPS
    return out - np.log(N) / EPS

@@ -1,0 +1,313 @@
+import math
+from contextlib import ExitStack
+
+import concourse.mybir as mybir
+from concourse.masks import make_identity
+
+FLOPS = 2 * 1024 * 1024 * 4096
+
+BF16 = mybir.dt.bfloat16
+F32 = mybir.dt.float32
+U32 = mybir.dt.uint32
+U8 = mybir.dt.uint8
+FP8X4 = mybir.dt.float8_e4m3fn_x4
+ALU = mybir.AluOpType
+ACT = mybir.ActivationFunctionType
+AX = mybir.AxisListType
+
+P = 128
+
+
+def tile_mex_t_kernel(tc, x, offsets, out):
+    nc = tc.nc
+    with ExitStack() as ctx:
+        keep = ctx.enter_context(tc.tile_pool(name="keep", bufs=1))
+        dpool = ctx.enter_context(tc.tile_pool(name="dpool", bufs=3))
+        epool = ctx.enter_context(tc.tile_pool(name="epool", bufs=3))
+        gpool = ctx.enter_context(tc.tile_pool(name="gpool", bufs=2))
+        opool = ctx.enter_context(tc.tile_pool(name="opool", bufs=3))
+        pm = ctx.enter_context(tc.psum_pool(name="pm", bufs=1))
+        pw = ctx.enter_context(tc.psum_pool(name="pw", bufs=4))
+        ctx.enter_context(tc.manual_schedule())
+
+        xf = x.rearrange("i c h w -> (i c) (h w)")
+        bv = offsets.rearrange("o (p mt) c h w -> p (o mt) (c h w)", mt=8)
+        ov = out.rearrange("i (p mt) h w -> i p mt (h w)", mt=8)
+
+        ident = keep.tile([P, P], BF16)
+        nsel = keep.tile([P, 4, P], BF16)
+        b_sb = keep.tile([P, 8, 1024], BF16)
+        tr1 = keep.tile([P, 2, 512], BF16)
+        tr2 = keep.tile([P, 2, 256], BF16)
+        nmb = keep.tile([P, 8], F32)
+        mbc = keep.tile([P, 8], F32)
+        ebp = keep.tile([P, 8, 1024], BF16)
+        ebc = keep.tile([P, 2, 1024], U32, align_bytes=64)
+        ebs = keep.tile([P, 2, 1024], U8, align_bytes=64)
+        xc0 = keep.tile([P, 1225], BF16)
+        xc1 = keep.tile([P, 1225], BF16)
+        xc = [xc0, xc1]
+        t1 = keep.tile([P, 1225], BF16)
+        t2 = keep.tile([P, 1225], BF16)
+        t3 = keep.tile([P, 1225], BF16)
+        p4 = keep.tile([P, 1024], BF16)
+        mt_col = keep.tile([P, 2, 16], BF16)
+        xs = keep.tile([P, 2, 4, 1120], BF16)
+        mxs = keep.tile([P, 4, 1024], BF16)
+        exc = keep.tile([P, 2, 4096], U32, align_bytes=64)
+        exs = keep.tile([P, 2, 4096], U8, align_bytes=64)
+        mxp0 = pm.tile([P, 1024], BF16)
+        mxp1 = pm.tile([P, 1024], BF16)
+        mxp2 = pm.tile([P, 1024], BF16)
+        mxp3 = pm.tile([P, 1024], BF16)
+        mxp = [mxp0, mxp1, mxp2, mxp3]
+
+        def load_x_rows(pr):
+            for g in range(2):
+                for dh in range(4):
+                    nc.sync.dma_start(
+                        out=xs[dh:P:4, g, 2 * pr : 2 * pr + 2, :],
+                        in_=x[2 * pr : 2 * pr + 2, 32 * g : 32 * g + 32, dh : dh + 32, :].rearrange(
+                            "i c h w -> c i (h w)"
+                        ),
+                    )
+
+        def max_of_b(q):
+            s = slice(2 * q, 2 * q + 2)
+            nc.vector.tensor_max(out=tr1[:], in0=b_sb[:, s, 0:512], in1=b_sb[:, s, 512:1024])
+            nc.vector.tensor_max(out=tr2[:], in0=tr1[:, :, 0:256], in1=tr1[:, :, 256:512])
+            nc.vector.tensor_reduce(out=nmb[:, s], in_=tr2[:], axis=AX.X, op=ALU.max, negate=True)
+
+        def exp_of_b(mt):
+            nc.scalar.activation(
+                out=ebp[:, mt, :].rearrange("m (g t p) -> m g t p", g=2, t=4),
+                in_=b_sb[:, mt, :].rearrange("m (g p t) -> m g t p", g=2, t=4),
+                func=ACT.Exp,
+                bias=nmb[:, mt : mt + 1],
+                scale=1.0,
+            )
+
+        def pool_a(pr):
+            nc.vector.tensor_max(out=t1[:, 0:1224], in0=xc[pr][:, 0:1224], in1=xc[pr][:, 1:1225])
+            nc.vector.tensor_max(out=t2[:, 0:1222], in0=t1[:, 0:1222], in1=t1[:, 2:1224])
+
+        def pool_b(pr):
+            nc.vector.tensor_max(out=t3[:, 0:1187], in0=t2[:, 0:1187], in1=t2[:, 35:1222])
+            nc.vector.tensor_max(
+                out=p4[:].rearrange("p (h w) -> p h w", w=32),
+                in0=t3[:, 0:1120].rearrange("p (h w) -> p h w", w=35)[:, :, 0:32],
+                in1=t3[:, 70:1190].rearrange("p (h w) -> p h w", w=35)[:, :, 0:32],
+            )
+
+        def max_over_channels(pr):
+            pt = pw.tile([P, 8, P], BF16, tag="w", name="pt")
+            for j in range(8):
+                nc.tensor.transpose(pt[:, j, :], p4[:, j * P : (j + 1) * P], ident[:])
+            with nc.allow_low_precision(reason="a maximum of bfloat16 values is a bfloat16 value"):
+                nc.vector.tensor_reduce(
+                    out=mt_col[:, pr, :],
+                    in_=pt[:].rearrange("p j (il c) -> p (j il) c", c=64),
+                    axis=AX.X,
+                    op=ALU.max,
+                )
+
+        def m_col(i, j):
+            k = 2 * j + i % 2
+            return mt_col[:, i // 2, k : k + 1].to_broadcast([P, P])
+
+        def spread_mx(i):
+            for j in range(8):
+                nc.tensor.matmul(
+                    out=mxp[i][:, j * P : (j + 1) * P], lhsT=m_col(i, j), rhs=ident[:], start=True, stop=True
+                )
+
+        def copy_mx(i):
+            nc.vector.tensor_copy(out=mxs[:, i, :], in_=mxp[i][:])
+
+        def chunk_on_pe(g, i, c, e_tile):
+            hh, b = c // 4, c % 4
+            dps = pw.tile([P, 512], F32, tag="w", name="dps")
+            rows = xs[:, g, i, :].rearrange("p (h w) -> p h w", w=35)
+            for jj in range(4):
+                h0 = 16 * hh + 4 * jj
+                o = dps[:, jj * P : (jj + 1) * P]
+                nc.tensor.matmul(
+                    out=o.rearrange("p (r w) -> p r w", w=32),
+                    lhsT=ident[:],
+                    rhs=rows[:, h0 : h0 + 4, b : b + 32],
+                    start=True,
+                    stop=False,
+                )
+                nc.tensor.matmul(out=o, lhsT=m_col(i, 4 * hh + jj), rhs=nsel[:, b, :], start=False, stop=True)
+            nc.scalar.activation(out=e_tile[:, c * 512 : (c + 1) * 512], in_=dps[:], func=ACT.Exp)
+
+        def subtract(eng, g, i, b, d_tile, m_ap):
+            eng.tensor_tensor(
+                out=d_tile[:].rearrange("p (hh bb hl a d) -> p hh bb hl a d", hh=2, bb=4, hl=16, a=8)[:, :, b],
+                in0=xs[:, g, i, :]
+                .rearrange("p (hh hl w) -> p hh hl w", hh=2, w=35)[:, :, :, b : b + 32]
+                .rearrange("p hh hl (a d) -> p hh hl a d", d=4),
+                in1=m_ap.rearrange("p (hh hl a bb) -> p hh hl a bb", hh=2, hl=16, bb=4)[:, :, :, :, b]
+                .unsqueeze(4)
+                .to_broadcast([P, 2, 16, 8, 4]),
+                op=ALU.subtract,
+            )
+
+        def quantise_ex(g, i, e_tile):
+            nc.vector.quantize_mx(
+                out=exc[:, g, i * 1024 : (i + 1) * 1024].bitcast(FP8X4),
+                scales=exs[:, g, i * 1024 : (i + 1) * 1024],
+                in_=e_tile[:],
+            )
+
+        def transpose_eb(mt):
+            et = pw.tile([P, 8, P], BF16, tag="w", name="et")
+            for gt in range(8):
+                nc.tensor.transpose(et[:, gt, :], ebp[:, mt, gt * P : (gt + 1) * P], ident[:])
+            return et
+
+        def regroup_eb(mt, et, ebg):
+            ml = mt % 2
+            nc.vector.tensor_copy(
+                out=ebg[:, :, ml * P : (ml + 1) * P, :], in_=et[:].rearrange("p (g t) m -> p g m t", g=2)
+            )
+
+        def quantise_eb(mp, ebg):
+            for g in range(2):
+                nc.vector.quantize_mx(
+                    out=ebc[:, g, mp * 256 : (mp + 1) * 256].bitcast(FP8X4),
+                    scales=ebs[:, g, mp * 256 : (mp + 1) * 256],
+                    in_=ebg[:, g].rearrange("p m t -> p (m t)"),
+                )
+
+        make_identity(nc, ident[:])
+        for b in range(4):
+            nc.vector.tensor_scalar_mul(
+                out=nsel[:, b, :].rearrange("p (r a d) -> p r a d", a=8, d=4),
+                in0=ident[:]
+                .rearrange("p (r a bb) -> p r a bb", a=8, bb=4)[:, :, :, b]
+                .unsqueeze(3)
+                .to_broadcast([P, 4, 8, 4]),
+                scalar1=-1.0,
+            )
+
+        nc.sync.dma_start(out=b_sb[:, 0:2, :], in_=bv[:, 0:2, :])
+        nc.sync.dma_start(out=xc[0][:], in_=xf[0:P, :])
+        for q in range(1, 4):
+            nc.sync.dma_start(out=b_sb[:, 2 * q : 2 * q + 2, :], in_=bv[:, 2 * q : 2 * q + 2, :])
+        load_x_rows(0)
+        nc.sync.dma_start(out=xc[1][:], in_=xf[P : 2 * P, :])
+        load_x_rows(1)
+
+        for q in range(4):
+            max_of_b(q)
+            exp_of_b(2 * q)
+            exp_of_b(2 * q + 1)
+        nc.vector.tensor_scalar(
+            out=mbc[:], in0=nmb[:], scalar1=-1.0, scalar2=-math.log(1024.0), op0=ALU.mult, op1=ALU.add
+        )
+
+        pool_a(0)
+        pool_b(0)
+        max_over_channels(0)
+
+        units = [(g, i) for i in range(4) for g in range(2)]
+        d_tiles = {}
+        e_tiles = {}
+
+        def gp_subs(u):
+            g, i = units[u]
+            d_tiles[u] = dpool.tile([P, 4096], F32, name="dt")
+            subtract(nc.gpsimd, g, i, 0, d_tiles[u], mxs[:, i, :])
+            subtract(nc.gpsimd, g, i, 1, d_tiles[u], mxs[:, i, :])
+
+        def dve_sub(u, b):
+            g, i = units[u]
+            subtract(nc.vector, g, i, b, d_tiles[u], mxp[i][:])
+
+        e_tiles[0] = epool.tile([P, 4096], BF16, name="et_ex", align_bytes=64)
+        chunk_on_pe(0, 0, 0, e_tiles[0])
+        chunk_on_pe(0, 0, 1, e_tiles[0])
+        spread_mx(1)
+        pool_a(1)
+        copy_mx(1)
+        gp_subs(2)
+        for c in range(2, 8):
+            chunk_on_pe(0, 0, c, e_tiles[0])
+        pool_b(1)
+        dve_sub(2, 3)
+        max_over_channels(1)
+        dve_sub(2, 2)
+
+        e_tiles[1] = epool.tile([P, 4096], BF16, name="et_ex", align_bytes=64)
+        chunk_on_pe(1, 0, 0, e_tiles[1])
+        chunk_on_pe(1, 0, 1, e_tiles[1])
+        spread_mx(2)
+        spread_mx(3)
+        copy_mx(2)
+        copy_mx(3)
+        gp_subs(3)
+        for c in range(2, 8):
+            chunk_on_pe(1, 0, c, e_tiles[1])
+        spread_mx(0)
+        quantise_ex(0, 0, e_tiles[0])
+        quantise_ex(1, 0, e_tiles[1])
+        dve_sub(3, 3)
+        dve_sub(3, 2)
+
+        eb_plan = {2: [0], 3: [1], 4: [2], 5: [3], 6: [4, 5], 7: [6, 7]}
+        ebg_now = [None]
+        for u in range(2, 8):
+            g, i = units[u]
+            e_tiles[u] = epool.tile([P, 4096], BF16, name="et_ex", align_bytes=64)
+            for hh in range(2):
+                nc.scalar.activation(
+                    out=e_tiles[u][:, hh * 2048 : (hh + 1) * 2048],
+                    in_=d_tiles[u][:, hh * 2048 : (hh + 1) * 2048],
+                    func=ACT.Exp,
+                )
+            if u + 2 < 8:
+                gp_subs(u + 2)
+                dve_sub(u + 2, 3)
+                dve_sub(u + 2, 2)
+            quantise_ex(g, i, e_tiles[u])
+            for mt in eb_plan[u]:
+                et = transpose_eb(mt)
+                if mt % 2 == 0:
+                    ebg_now[0] = gpool.tile([P, 2, 256, 4], BF16, name="ebg", align_bytes=64)
+                regroup_eb(mt, et, ebg_now[0])
+                if mt % 2 == 1:
+                    quantise_eb(mt // 2, ebg_now[0])
+
+        for i in range(4):
+            for mp in range(4):
+                ot = opool.tile([P, 2, 1024], F32, name="ot")
+                for ml in range(2):
+                    mt = 2 * mp + ml
+                    for hh in range(2):
+                        acc = pw.tile([P, 512], F32, tag="w", name="acc")
+                        n0 = i * 1024 + hh * 512
+                        for g in range(2):
+                            nc.tensor.matmul_mx(
+                                out=acc[:],
+                                lhsT=ebc[:, g, mt * P : (mt + 1) * P].bitcast(FP8X4),
+                                lhsT_scale=ebs[:, g, mt * P : (mt + 1) * P],
+                                rhs=exc[:, g, n0 : n0 + 512].bitcast(FP8X4),
+                                rhs_scale=exs[:, g, n0 : n0 + 512],
+                                start=(g == 0),
+                                stop=(g == 1),
+                            )
+                        nc.scalar.activation(
+                            out=ot[:, ml, hh * 512 : (hh + 1) * 512].rearrange("p (hl a bb) -> p hl a bb", a=8, bb=4),
+                            in_=acc[:].rearrange("p (bb hl a) -> p hl a bb", bb=4, a=8),
+                            func=ACT.Ln,
+                        )
+                    nc.vector.scalar_tensor_tensor(
+                        out=ot[:, ml, :],
+                        in0=ot[:, ml, :],
+                        scalar=mbc[:, mt : mt + 1],
+                        in1=mxp[i][:],
+                        op0=ALU.add,
+                        op1=ALU.add,
+                    )
+                nc.sync.dma_start(out=ov[i][:, 2 * mp : 2 * mp + 2, :], in_=ot[:])

@@ -25,42 +25,46 @@ def tile_mex_t_kernel(tc, x, offsets, out):
         dpool = ctx.enter_context(tc.tile_pool(name="dpool", bufs=3))
         epool = ctx.enter_context(tc.tile_pool(name="epool", bufs=3))
         gpool = ctx.enter_context(tc.tile_pool(name="gpool", bufs=2))
-        opool = ctx.enter_context(tc.tile_pool(name="opool", bufs=3))
-        pm = ctx.enter_context(tc.psum_pool(name="pm", bufs=1))
-        pw = ctx.enter_context(tc.psum_pool(name="pw", bufs=4))
+        opool = ctx.enter_context(tc.tile_pool(name="opool", bufs=8))
+        ps = ctx.enter_context(tc.psum_pool(name="ps", bufs=1))
         ctx.enter_context(tc.manual_schedule())
 
-        xf = x.rearrange("i c h w -> (i c) (h w)")
+        xq_v = x.rearrange("i (ch cl) h w -> (i ch) cl (h w)", cl=2)
         bv = offsets.rearrange("o (p mt) c h w -> p (o mt) (c h w)", mt=8)
         ov = out.rearrange("i (p mt) h w -> i p mt (h w)", mt=8)
 
         ident = keep.tile([P, P], BF16)
+        ident32 = keep.tile([P, P], F32)
         nsel = keep.tile([P, 4, P], BF16)
         b_sb = keep.tile([P, 8, 1024], BF16)
-        tr1 = keep.tile([P, 2, 512], BF16)
-        tr2 = keep.tile([P, 2, 256], BF16)
+        tr1 = keep.tile([P, 4, 512], BF16)
+        tr2 = keep.tile([P, 4, 256], BF16)
+        tr3 = keep.tile([P, 4, 128], BF16)
         nmb = keep.tile([P, 8], F32)
         mbc = keep.tile([P, 8], F32)
         ebp = keep.tile([P, 8, 1024], BF16)
         ebc = keep.tile([P, 2, 1024], U32, align_bytes=64)
         ebs = keep.tile([P, 2, 1024], U8, align_bytes=64)
-        xc0 = keep.tile([P, 1225], BF16)
-        xc1 = keep.tile([P, 1225], BF16)
-        xc = [xc0, xc1]
-        t1 = keep.tile([P, 1225], BF16)
-        t2 = keep.tile([P, 1225], BF16)
-        t3 = keep.tile([P, 1225], BF16)
-        p4 = keep.tile([P, 1024], BF16)
-        mt_col = keep.tile([P, 2, 16], BF16)
-        xs = keep.tile([P, 2, 4, 1120], BF16)
+        xq = keep.tile([P, 2, 1225], BF16)
+        t0 = keep.tile([P, 665], BF16)
+        t1 = keep.tile([P, 665], BF16)
+        t2 = keep.tile([P, 665], BF16)
+        t3 = keep.tile([P, 665], BF16)
+        p4 = keep.tile([P, 2, 512], BF16)
+        mt_col = keep.tile([P, 2, 32], BF16)
+        negm = keep.tile([P, 2, 4, 32], F32)
         mxs = keep.tile([P, 4, 1024], BF16)
-        exc = keep.tile([P, 2, 4096], U32, align_bytes=64)
-        exs = keep.tile([P, 2, 4096], U8, align_bytes=64)
-        mxp0 = pm.tile([P, 1024], BF16)
-        mxp1 = pm.tile([P, 1024], BF16)
-        mxp2 = pm.tile([P, 1024], BF16)
-        mxp3 = pm.tile([P, 1024], BF16)
+        xs = keep.tile([P, 2, 4, 1120], BF16)
+        exc = keep.tile([P, 8, 2, 512], U32, align_bytes=64)
+        exs = keep.tile([P, 8, 2, 512], U8, align_bytes=64)
+        mxp0 = ps.tile([P, 1024], BF16)
+        mxp1 = ps.tile([P, 1024], BF16)
+        mxp2 = ps.tile([P, 1024], BF16)
+        mxp3 = ps.tile([P, 1024], BF16)
         mxp = [mxp0, mxp1, mxp2, mxp3]
+
+        def bank(k, shape, dtype):
+            return ps.tile(shape, dtype, tag="bank%d" % k, name="bk%d" % k)
 
         def load_x_rows(pr):
             for g in range(2):
@@ -72,11 +76,12 @@ def tile_mex_t_kernel(tc, x, offsets, out):
                         ),
                     )
 
-        def max_of_b(q):
-            s = slice(2 * q, 2 * q + 2)
-            nc.vector.tensor_max(out=tr1[:], in0=b_sb[:, s, 0:512], in1=b_sb[:, s, 512:1024])
-            nc.vector.tensor_max(out=tr2[:], in0=tr1[:, :, 0:256], in1=tr1[:, :, 256:512])
-            nc.vector.tensor_reduce(out=nmb[:, s], in_=tr2[:], axis=AX.X, op=ALU.max, negate=True)
+        def max_of_b(m0, n):
+            s = slice(m0, m0 + n)
+            nc.vector.tensor_max(out=tr1[:, 0:n, :], in0=b_sb[:, s, 0:512], in1=b_sb[:, s, 512:1024])
+            nc.vector.tensor_max(out=tr2[:, 0:n, :], in0=tr1[:, 0:n, 0:256], in1=tr1[:, 0:n, 256:512])
+            nc.vector.tensor_max(out=tr3[:, 0:n, :], in0=tr2[:, 0:n, 0:128], in1=tr2[:, 0:n, 128:256])
+            nc.vector.tensor_reduce(out=nmb[:, s], in_=tr3[:, 0:n, :], axis=AX.X, op=ALU.max, negate=True)
 
         def exp_of_b(mt):
             nc.scalar.activation(
@@ -87,81 +92,108 @@ def tile_mex_t_kernel(tc, x, offsets, out):
                 scale=1.0,
             )
 
-        def pool_a(pr):
-            nc.vector.tensor_max(out=t1[:, 0:1224], in0=xc[pr][:, 0:1224], in1=xc[pr][:, 1:1225])
-            nc.vector.tensor_max(out=t2[:, 0:1222], in0=t1[:, 0:1222], in1=t1[:, 2:1224])
+        def pool_a(hh):
+            f0 = 560 * hh
+            nc.vector.tensor_max(out=t0[:], in0=xq[:, 0, f0 : f0 + 665], in1=xq[:, 1, f0 : f0 + 665])
+            nc.vector.tensor_max(out=t1[:, 0:664], in0=t0[:, 0:664], in1=t0[:, 1:665])
+            nc.vector.tensor_max(out=t2[:, 0:662], in0=t1[:, 0:662], in1=t1[:, 2:664])
 
-        def pool_b(pr):
-            nc.vector.tensor_max(out=t3[:, 0:1187], in0=t2[:, 0:1187], in1=t2[:, 35:1222])
+        def pool_b(hh):
+            nc.vector.tensor_max(out=t3[:, 0:627], in0=t2[:, 0:627], in1=t2[:, 35:662])
             nc.vector.tensor_max(
-                out=p4[:].rearrange("p (h w) -> p h w", w=32),
-                in0=t3[:, 0:1120].rearrange("p (h w) -> p h w", w=35)[:, :, 0:32],
-                in1=t3[:, 70:1190].rearrange("p (h w) -> p h w", w=35)[:, :, 0:32],
+                out=p4[:, hh, :].rearrange("p (h w) -> p h w", w=32),
+                in0=t3[:, 0:560].rearrange("p (h w) -> p h w", w=35)[:, :, 0:32],
+                in1=t3[:, 70:630].rearrange("p (h w) -> p h w", w=35)[:, :, 0:32],
             )
 
-        def max_over_channels(pr):
-            pt = pw.tile([P, 8, P], BF16, tag="w", name="pt")
-            for j in range(8):
-                nc.tensor.transpose(pt[:, j, :], p4[:, j * P : (j + 1) * P], ident[:])
+        def transpose_pooled(hh):
+            pt = bank(3, [P, 4, P], BF16)
+            for jj in range(4):
+                nc.tensor.transpose(pt[:, jj, :], p4[:, hh, jj * P : (jj + 1) * P], ident[:])
+            return pt
+
+        def max_over_channels(hh, pt):
             with nc.allow_low_precision(reason="a maximum of bfloat16 values is a bfloat16 value"):
                 nc.vector.tensor_reduce(
-                    out=mt_col[:, pr, :],
-                    in_=pt[:].rearrange("p j (il c) -> p (j il) c", c=64),
+                    out=mt_col[:, hh, 0:16],
+                    in_=pt[:].rearrange("p j (i c) -> p (j i) c", c=32),
                     axis=AX.X,
                     op=ALU.max,
                 )
 
-        def m_col(i, j):
-            k = 2 * j + i % 2
-            return mt_col[:, i // 2, k : k + 1].to_broadcast([P, P])
+        def select_negated(hh):
+            selp = bank(3, [P, 4, 32], F32)
+            for b in range(4):
+                nc.tensor.matmul(out=selp[:, b, :], lhsT=nsel[:, b, :], rhs=mt_col[:, hh, :], start=True, stop=True)
+            return selp
 
-        def spread_mx(i):
-            for j in range(8):
-                nc.tensor.matmul(
-                    out=mxp[i][:, j * P : (j + 1) * P], lhsT=m_col(i, j), rhs=ident[:], start=True, stop=True
-                )
+        def copy_negated(hh, selp):
+            nc.vector.tensor_copy(out=negm[:, hh], in_=selp[:])
 
-        def copy_mx(i):
-            nc.vector.tensor_copy(out=mxs[:, i, :], in_=mxp[i][:])
-
-        def chunk_on_pe(g, i, c, e_tile):
-            hh, b = c // 4, c % 4
-            dps = pw.tile([P, 512], F32, tag="w", name="dps")
-            rows = xs[:, g, i, :].rearrange("p (h w) -> p h w", w=35)
+        def spread_mx(hh, i):
             for jj in range(4):
-                h0 = 16 * hh + 4 * jj
-                o = dps[:, jj * P : (jj + 1) * P]
-                nc.tensor.matmul(
-                    out=o.rearrange("p (r w) -> p r w", w=32),
-                    lhsT=ident[:],
-                    rhs=rows[:, h0 : h0 + 4, b : b + 32],
-                    start=True,
-                    stop=False,
+                k = 4 * jj + i
+                j = 4 * hh + jj
+                nc.tensor.transpose(
+                    mxp[i][:, j * P : (j + 1) * P], mt_col[:, hh, k : k + 1].to_broadcast([P, P]), ident[:]
                 )
-                nc.tensor.matmul(out=o, lhsT=m_col(i, 4 * hh + jj), rhs=nsel[:, b, :], start=False, stop=True)
-            nc.scalar.activation(out=e_tile[:, c * 512 : (c + 1) * 512], in_=dps[:], func=ACT.Exp)
 
-        def subtract(eng, g, i, b, d_tile, m_ap):
+        def copy_mx(hh, i):
+            s = slice(hh * 512, (hh + 1) * 512)
+            nc.vector.tensor_copy(out=mxs[:, i, s], in_=mxp[i][:, s])
+
+        chunk_no = [0]
+
+        def chunk_on_pe(g, i, hh, b, e_tile):
+            dps = bank(chunk_no[0] % 3, [P, 512], F32)
+            chunk_no[0] += 1
+            rows = xs[:, g, i, :].rearrange("p (h w) -> p h w", w=35)
+            nc.tensor.matmul(
+                out=dps[:].rearrange("p (r w) -> p r w", w=32),
+                lhsT=ident[:],
+                rhs=rows[:, 16 * hh : 16 * hh + 16, b : b + 32],
+                start=True,
+                stop=False,
+            )
+            for jj in range(4):
+                k = 4 * jj + i
+                nc.tensor.matmul(
+                    out=dps[:, jj * P : (jj + 1) * P],
+                    lhsT=negm[:, hh, b, k : k + 1].to_broadcast([P, P]),
+                    rhs=ident32[:],
+                    is_transpose=True,
+                    start=False,
+                    stop=(jj == 3),
+                )
+            nc.scalar.activation(out=e_tile[:, g, b * 512 : (b + 1) * 512], in_=dps[:], func=ACT.Exp)
+
+        def subtract(eng, g, i, hh, b, d_tile):
             eng.tensor_tensor(
-                out=d_tile[:].rearrange("p (hh bb hl a d) -> p hh bb hl a d", hh=2, bb=4, hl=16, a=8)[:, :, b],
+                out=d_tile[:, g, b - 2, :].rearrange("p (hl a d) -> p hl a d", a=8, d=4),
                 in0=xs[:, g, i, :]
-                .rearrange("p (hh hl w) -> p hh hl w", hh=2, w=35)[:, :, :, b : b + 32]
-                .rearrange("p hh hl (a d) -> p hh hl a d", d=4),
-                in1=m_ap.rearrange("p (hh hl a bb) -> p hh hl a bb", hh=2, hl=16, bb=4)[:, :, :, :, b]
-                .unsqueeze(4)
-                .to_broadcast([P, 2, 16, 8, 4]),
+                .rearrange("p (h w) -> p h w", w=35)[:, 16 * hh : 16 * hh + 16, b : b + 32]
+                .rearrange("p hl (a d) -> p hl a d", d=4),
+                in1=mxs[:, i, hh * 512 : (hh + 1) * 512]
+                .rearrange("p (hl a bb) -> p hl a bb", a=8, bb=4)[:, :, :, b]
+                .unsqueeze(3)
+                .to_broadcast([P, 16, 8, 4]),
                 op=ALU.subtract,
             )
 
-        def quantise_ex(g, i, e_tile):
+        def exp_piece(g, d_tile, e_tile):
+            nc.scalar.activation(
+                out=e_tile[:, g, 1024:2048], in_=d_tile[:, g].rearrange("p b n -> p (b n)"), func=ACT.Exp
+            )
+
+        def quantise_ex(hh, i, e_tile):
             nc.vector.quantize_mx(
-                out=exc[:, g, i * 1024 : (i + 1) * 1024].bitcast(FP8X4),
-                scales=exs[:, g, i * 1024 : (i + 1) * 1024],
-                in_=e_tile[:],
+                out=exc[:, 2 * i + hh].rearrange("p g n -> p (g n)").bitcast(FP8X4),
+                scales=exs[:, 2 * i + hh].rearrange("p g n -> p (g n)"),
+                in_=e_tile[:].rearrange("p g n -> p (g n)"),
             )
 
         def transpose_eb(mt):
-            et = pw.tile([P, 8, P], BF16, tag="w", name="et")
+            et = bank(3, [P, 8, P], BF16)
             for gt in range(8):
                 nc.tensor.transpose(et[:, gt, :], ebp[:, mt, gt * P : (gt + 1) * P], ident[:])
             return et
@@ -181,6 +213,8 @@ def tile_mex_t_kernel(tc, x, offsets, out):
                 )
 
         make_identity(nc, ident[:])
+        nc.vector.memset(mt_col[:], 0.0)
+        nc.vector.tensor_copy(out=ident32[:], in_=ident[:])
         for b in range(4):
             nc.vector.tensor_scalar_mul(
                 out=nsel[:, b, :].rearrange("p (r a d) -> p r a d", a=8, d=4),
@@ -191,123 +225,141 @@ def tile_mex_t_kernel(tc, x, offsets, out):
                 scalar1=-1.0,
             )
 
-        nc.sync.dma_start(out=b_sb[:, 0:2, :], in_=bv[:, 0:2, :])
-        nc.sync.dma_start(out=xc[0][:], in_=xf[0:P, :])
-        for q in range(1, 4):
-            nc.sync.dma_start(out=b_sb[:, 2 * q : 2 * q + 2, :], in_=bv[:, 2 * q : 2 * q + 2, :])
+        nc.sync.dma_start(out=b_sb[:, 0:1, :], in_=bv[:, 0:1, :])
+        nc.sync.dma_start(out=b_sb[:, 1:2, :], in_=bv[:, 1:2, :])
+        nc.sync.dma_start(out=b_sb[:, 2:4, :], in_=bv[:, 2:4, :])
+        nc.sync.dma_start(out=xq[:], in_=xq_v)
+        nc.sync.dma_start(out=b_sb[:, 4:6, :], in_=bv[:, 4:6, :])
+        nc.sync.dma_start(out=b_sb[:, 6:8, :], in_=bv[:, 6:8, :])
         load_x_rows(0)
-        nc.sync.dma_start(out=xc[1][:], in_=xf[P : 2 * P, :])
         load_x_rows(1)
 
-        for q in range(4):
-            max_of_b(q)
-            exp_of_b(2 * q)
-            exp_of_b(2 * q + 1)
+        max_of_b(0, 1)
+        exp_of_b(0)
+        max_of_b(1, 1)
+        exp_of_b(1)
+        max_of_b(2, 2)
+        exp_of_b(2)
+        exp_of_b(3)
+        pool_a(0)
+        max_of_b(4, 2)
+        exp_of_b(4)
+        exp_of_b(5)
+        pool_b(0)
+        pt0 = transpose_pooled(0)
+        max_of_b(6, 2)
+        exp_of_b(6)
+        exp_of_b(7)
+        max_over_channels(0, pt0)
+        sp0 = select_negated(0)
+        copy_negated(0, sp0)
+
+        units = [(hh, i) for hh in range(2) for i in range(4)]
+        d_tiles = {}
+        e_tiles = {}
+        ebg_now = [None]
+
+        def prepare(u):
+            hh, i = units[u]
+            d_tile = dpool.tile([P, 2, 2, 512], F32, name="dt")
+            d_tiles[u] = d_tile
+            subtract(nc.vector, 0, i, hh, 2, d_tile)
+            subtract(nc.vector if u == 0 else nc.gpsimd, 0, i, hh, 3, d_tile)
+            subtract(nc.gpsimd, 1, i, hh, 2, d_tile)
+            subtract(nc.gpsimd, 1, i, hh, 3, d_tile)
+
+        def chunks(u, g):
+            hh, i = units[u]
+            chunk_on_pe(g, i, hh, 0, e_tiles[u])
+            chunk_on_pe(g, i, hh, 1, e_tiles[u])
+
+        def eb_codes(mt):
+            et = transpose_eb(mt)
+            if mt % 2 == 0:
+                ebg_now[0] = gpool.tile([P, 2, 256, 4], BF16, name="ebg", align_bytes=64)
+            regroup_eb(mt, et, ebg_now[0])
+            if mt % 2 == 1:
+                quantise_eb(mt // 2, ebg_now[0])
+
+        spread_mx(0, 0)
+        spread_mx(0, 1)
+        copy_mx(0, 0)
+        prepare(0)
+        for u in range(8):
+            hh, i = units[u]
+            e_tiles[u] = epool.tile([P, 2, 2048], BF16, name="et_ex", align_bytes=64)
+            chunks(u, 0)
+            if u == 0:
+                chunks(u, 1)
+                spread_mx(0, 2)
+                spread_mx(0, 3)
+                copy_mx(0, 1)
+                prepare(1)
+                exp_piece(0, d_tiles[u], e_tiles[u])
+                copy_mx(0, 2)
+                copy_mx(0, 3)
+                pool_a(1)
+                pool_b(1)
+            else:
+                exp_piece(0, d_tiles[u], e_tiles[u])
+                if u == 2:
+                    sp1 = select_negated(1)
+                    copy_negated(1, sp1)
+                if u == 7:
+                    eb_codes(6)
+                chunks(u, 1)
+                if u + 1 < 8:
+                    prepare(u + 1)
+            exp_piece(1, d_tiles[u], e_tiles[u])
+            if u == 0:
+                eb_codes(0)
+            if u == 1:
+                pt1 = transpose_pooled(1)
+                max_over_channels(1, pt1)
+            if u == 2:
+                for v in range(4):
+                    spread_mx(1, v)
+                for v in range(4):
+                    copy_mx(1, v)
+            if u >= 2:
+                eb_codes(u - 1 if u < 7 else 7)
+            quantise_ex(hh, i, e_tiles[u])
         nc.vector.tensor_scalar(
             out=mbc[:], in0=nmb[:], scalar1=-1.0, scalar2=-math.log(1024.0), op0=ALU.mult, op1=ALU.add
         )
 
-        pool_a(0)
-        pool_b(0)
-        max_over_channels(0)
-
-        units = [(g, i) for i in range(4) for g in range(2)]
-        d_tiles = {}
-        e_tiles = {}
-
-        def gp_subs(u):
-            g, i = units[u]
-            d_tiles[u] = dpool.tile([P, 4096], F32, name="dt")
-            subtract(nc.gpsimd, g, i, 0, d_tiles[u], mxs[:, i, :])
-            subtract(nc.gpsimd, g, i, 1, d_tiles[u], mxs[:, i, :])
-
-        def dve_sub(u, b):
-            g, i = units[u]
-            subtract(nc.vector, g, i, b, d_tiles[u], mxp[i][:])
-
-        e_tiles[0] = epool.tile([P, 4096], BF16, name="et_ex", align_bytes=64)
-        chunk_on_pe(0, 0, 0, e_tiles[0])
-        chunk_on_pe(0, 0, 1, e_tiles[0])
-        spread_mx(1)
-        pool_a(1)
-        copy_mx(1)
-        gp_subs(2)
-        for c in range(2, 8):
-            chunk_on_pe(0, 0, c, e_tiles[0])
-        pool_b(1)
-        dve_sub(2, 3)
-        max_over_channels(1)
-        dve_sub(2, 2)
-
-        e_tiles[1] = epool.tile([P, 4096], BF16, name="et_ex", align_bytes=64)
-        chunk_on_pe(1, 0, 0, e_tiles[1])
-        chunk_on_pe(1, 0, 1, e_tiles[1])
-        spread_mx(2)
-        spread_mx(3)
-        copy_mx(2)
-        copy_mx(3)
-        gp_subs(3)
-        for c in range(2, 8):
-            chunk_on_pe(1, 0, c, e_tiles[1])
-        spread_mx(0)
-        quantise_ex(0, 0, e_tiles[0])
-        quantise_ex(1, 0, e_tiles[1])
-        dve_sub(3, 3)
-        dve_sub(3, 2)
-
-        eb_plan = {2: [0], 3: [1], 4: [2], 5: [3], 6: [4, 5], 7: [6, 7]}
-        ebg_now = [None]
-        for u in range(2, 8):
-            g, i = units[u]
-            e_tiles[u] = epool.tile([P, 4096], BF16, name="et_ex", align_bytes=64)
-            for hh in range(2):
-                nc.scalar.activation(
-                    out=e_tiles[u][:, hh * 2048 : (hh + 1) * 2048],
-                    in_=d_tiles[u][:, hh * 2048 : (hh + 1) * 2048],
-                    func=ACT.Exp,
-                )
-            if u + 2 < 8:
-                gp_subs(u + 2)
-                dve_sub(u + 2, 3)
-                dve_sub(u + 2, 2)
-            quantise_ex(g, i, e_tiles[u])
-            for mt in eb_plan[u]:
-                et = transpose_eb(mt)
-                if mt % 2 == 0:
-                    ebg_now[0] = gpool.tile([P, 2, 256, 4], BF16, name="ebg", align_bytes=64)
-                regroup_eb(mt, et, ebg_now[0])
-                if mt % 2 == 1:
-                    quantise_eb(mt // 2, ebg_now[0])
-
+        acc_no = [0]
         for i in range(4):
-            for mp in range(4):
-                ot = opool.tile([P, 2, 1024], F32, name="ot")
-                for ml in range(2):
-                    mt = 2 * mp + ml
-                    for hh in range(2):
-                        acc = pw.tile([P, 512], F32, tag="w", name="acc")
-                        n0 = i * 1024 + hh * 512
-                        for g in range(2):
-                            nc.tensor.matmul_mx(
-                                out=acc[:],
-                                lhsT=ebc[:, g, mt * P : (mt + 1) * P].bitcast(FP8X4),
-                                lhsT_scale=ebs[:, g, mt * P : (mt + 1) * P],
-                                rhs=exc[:, g, n0 : n0 + 512].bitcast(FP8X4),
-                                rhs_scale=exs[:, g, n0 : n0 + 512],
-                                start=(g == 0),
-                                stop=(g == 1),
-                            )
-                        nc.scalar.activation(
-                            out=ot[:, ml, hh * 512 : (hh + 1) * 512].rearrange("p (hl a bb) -> p hl a bb", a=8, bb=4),
-                            in_=acc[:].rearrange("p (bb hl a) -> p hl a bb", bb=4, a=8),
-                            func=ACT.Ln,
+            for mt in range(8):
+                ot = opool.tile([P, 1024], F32, name="ot")
+                last = i == 3 and mt == 7
+                for hh in range(2):
+                    acc = bank(acc_no[0] % 4, [P, 512], F32)
+                    acc_no[0] += 1
+                    for g in range(2):
+                        nc.tensor.matmul_mx(
+                            out=acc[:],
+                            lhsT=ebc[:, g, mt * P : (mt + 1) * P].bitcast(FP8X4),
+                            lhsT_scale=ebs[:, g, mt * P : (mt + 1) * P],
+                            rhs=exc[:, 2 * i + hh, g, :].bitcast(FP8X4),
+                            rhs_scale=exs[:, 2 * i + hh, g, :],
+                            start=(g == 0),
+                            stop=(g == 1),
                         )
-                    nc.vector.scalar_tensor_tensor(
-                        out=ot[:, ml, :],
-                        in0=ot[:, ml, :],
-                        scalar=mbc[:, mt : mt + 1],
-                        in1=mxp[i][:],
-                        op0=ALU.add,
-                        op1=ALU.add,
+                    nc.scalar.activation(
+                        out=ot[:, hh * 512 : (hh + 1) * 512].rearrange("p (hl a bb) -> p hl a bb", a=8, bb=4),
+                        in_=acc[:].rearrange("p (bb hl a) -> p hl a bb", bb=4, a=8),
+                        func=ACT.Ln,
                     )
-                nc.sync.dma_start(out=ov[i][:, 2 * mp : 2 * mp + 2, :], in_=ot[:])
+                    if last:
+                        s = slice(hh * 512, (hh + 1) * 512)
+                        nc.vector.scalar_tensor_tensor(
+                            out=ot[:, s], in0=ot[:, s], scalar=mbc[:, mt : mt + 1], in1=mxp[i][:, s],
+                            op0=ALU.add, op1=ALU.add,
+                        )
+                        nc.sync.dma_start(out=ov[i][:, mt, s], in_=ot[:, s])
+                if not last:
+                    nc.vector.scalar_tensor_tensor(
+                        out=ot[:], in0=ot[:], scalar=mbc[:, mt : mt + 1], in1=mxp[i][:], op0=ALU.add, op1=ALU.add
+                    )
+                    nc.sync.dma_start(out=ov[i][:, mt, :], in_=ot[:])

@@ -22,7 +22,7 @@ def tile_mex_t_kernel(tc, x, offsets, out):
     nc = tc.nc
     with ExitStack() as ctx:
         keep = ctx.enter_context(tc.tile_pool(name="keep", bufs=1))
-        dpool = ctx.enter_context(tc.tile_pool(name="dpool", bufs=3))
+        dpool = ctx.enter_context(tc.tile_pool(name="dpool", bufs=4))
         epool = ctx.enter_context(tc.tile_pool(name="epool", bufs=3))
         gpool = ctx.enter_context(tc.tile_pool(name="gpool", bufs=2))
         opool = ctx.enter_context(tc.tile_pool(name="opool", bufs=8))
@@ -167,23 +167,40 @@ def tile_mex_t_kernel(tc, x, offsets, out):
                 )
             nc.scalar.activation(out=e_tile[:, g, b * 512 : (b + 1) * 512], in_=dps[:], func=ACT.Exp)
 
-        def subtract(eng, g, i, hh, b, d_tile):
-            eng.tensor_tensor(
-                out=d_tile[:, g, b - 2, :].rearrange("p (hl a d) -> p hl a d", a=8, d=4),
+        def subtract_on_vector(i, hh, g, b, dst):
+            nc.vector.tensor_tensor(
+                out=dst.rearrange("p (hl a d) -> p hl a d", a=8, d=4),
                 in0=xs[:, g, i, :]
                 .rearrange("p (h w) -> p h w", w=35)[:, 16 * hh : 16 * hh + 16, b : b + 32]
                 .rearrange("p hl (a d) -> p hl a d", d=4),
-                in1=mxs[:, i, hh * 512 : (hh + 1) * 512]
+                in1=mxp[i][:, hh * 512 : (hh + 1) * 512]
                 .rearrange("p (hl a bb) -> p hl a bb", a=8, bb=4)[:, :, :, b]
                 .unsqueeze(3)
                 .to_broadcast([P, 16, 8, 4]),
                 op=ALU.subtract,
             )
 
-        def exp_piece(g, d_tile, e_tile):
-            nc.scalar.activation(
-                out=e_tile[:, g, 1024:2048], in_=d_tile[:, g].rearrange("p b n -> p (b n)"), func=ACT.Exp
+        def subtract_on_gpsimd(i, hh, d_tile):
+            nc.gpsimd.tensor_tensor(
+                out=d_tile[:, 1:3, :].rearrange("p g (hl a d) -> p g hl a d", a=8, d=4),
+                in0=xs[:, :, i, :]
+                .rearrange("p g (h w) -> p g h w", w=35)[:, :, 16 * hh : 16 * hh + 16, 3:35]
+                .rearrange("p g hl (a d) -> p g hl a d", d=4),
+                in1=mxs[:, i, hh * 512 : (hh + 1) * 512]
+                .rearrange("p (hl a bb) -> p hl a bb", a=8, bb=4)[:, :, :, 3]
+                .unsqueeze(1)
+                .unsqueeze(4)
+                .to_broadcast([P, 2, 16, 8, 4]),
+                op=ALU.subtract,
             )
+
+        def exp_piece(g, d_tile, e_tile):
+            if g == 0:
+                nc.scalar.activation(
+                    out=e_tile[:, 0, 1024:2048], in_=d_tile[:, 0:2, :].rearrange("p b n -> p (b n)"), func=ACT.Exp
+                )
+            else:
+                nc.scalar.activation(out=e_tile[:, 1, 1536:2048], in_=d_tile[:, 2, :], func=ACT.Exp)
 
         def quantise_ex(hh, i, e_tile):
             nc.vector.quantize_mx(
@@ -259,19 +276,19 @@ def tile_mex_t_kernel(tc, x, offsets, out):
         e_tiles = {}
         ebg_now = [None]
 
-        def prepare(u):
+        def prepare_g(u):
             hh, i = units[u]
-            d_tile = dpool.tile([P, 2, 2, 512], F32, name="dt")
-            d_tiles[u] = d_tile
-            subtract(nc.vector, 0, i, hh, 2, d_tile)
-            subtract(nc.vector if u == 0 else nc.gpsimd, 0, i, hh, 3, d_tile)
-            subtract(nc.gpsimd, 1, i, hh, 2, d_tile)
-            subtract(nc.gpsimd, 1, i, hh, 3, d_tile)
+            d_tiles[u] = dpool.tile([P, 3, 512], F32, name="dt")
+            subtract_on_gpsimd(i, hh, d_tiles[u])
 
-        def chunks(u, g):
+        def prepare_v(u):
             hh, i = units[u]
-            chunk_on_pe(g, i, hh, 0, e_tiles[u])
-            chunk_on_pe(g, i, hh, 1, e_tiles[u])
+            subtract_on_vector(i, hh, 0, 2, d_tiles[u][:, 0, :])
+
+        def chunks(u, todo):
+            hh, i = units[u]
+            for g, b in todo:
+                chunk_on_pe(g, i, hh, b, e_tiles[u])
 
         def eb_codes(mt):
             et = transpose_eb(mt)
@@ -283,21 +300,26 @@ def tile_mex_t_kernel(tc, x, offsets, out):
 
         spread_mx(0, 0)
         spread_mx(0, 1)
-        copy_mx(0, 0)
-        prepare(0)
+        copy_mx(0, 1)
+        prepare_g(1)
+        d_tiles[0] = dpool.tile([P, 3, 512], F32, name="dt")
+        subtract_on_vector(0, 0, 0, 2, d_tiles[0][:, 0, :])
+        subtract_on_vector(0, 0, 0, 3, d_tiles[0][:, 1, :])
+        subtract_on_vector(0, 0, 1, 3, d_tiles[0][:, 2, :])
         for u in range(8):
             hh, i = units[u]
             e_tiles[u] = epool.tile([P, 2, 2048], BF16, name="et_ex", align_bytes=64)
-            chunks(u, 0)
+            chunks(u, [(0, 0), (0, 1)])
             if u == 0:
-                chunks(u, 1)
+                chunks(u, [(1, 0), (1, 1), (1, 2)])
                 spread_mx(0, 2)
                 spread_mx(0, 3)
-                copy_mx(0, 1)
-                prepare(1)
-                exp_piece(0, d_tiles[u], e_tiles[u])
                 copy_mx(0, 2)
+                prepare_g(2)
                 copy_mx(0, 3)
+                prepare_g(3)
+                prepare_v(1)
+                exp_piece(0, d_tiles[u], e_tiles[u])
                 pool_a(1)
                 pool_b(1)
             else:
@@ -307,20 +329,25 @@ def tile_mex_t_kernel(tc, x, offsets, out):
                     copy_negated(1, sp1)
                 if u == 7:
                     eb_codes(6)
-                chunks(u, 1)
-                if u + 1 < 8:
-                    prepare(u + 1)
+                chunks(u, [(1, 0), (1, 1), (1, 2)])
+                if u == 1:
+                    prepare_v(2)
+                    prepare_v(3)
             exp_piece(1, d_tiles[u], e_tiles[u])
             if u == 0:
                 eb_codes(0)
             if u == 1:
                 pt1 = transpose_pooled(1)
                 max_over_channels(1, pt1)
-            if u == 2:
-                for v in range(4):
+            if u == 2 or u == 3:
+                for v in (2 * u - 4, 2 * u - 3):
                     spread_mx(1, v)
-                for v in range(4):
+                for v in (2 * u - 4, 2 * u - 3):
                     copy_mx(1, v)
+            if 2 <= u < 6:
+                prepare_g(u + 2)
+            if 3 <= u < 7:
+                prepare_v(u + 1)
             if u >= 2:
                 eb_codes(u - 1 if u < 7 else 7)
             quantise_ex(hh, i, e_tiles[u])

@@ -36,6 +36,7 @@ def tile_mex_t_kernel(tc, x, offsets, out):
         ident = keep.tile([P, P], BF16)
         ident32 = keep.tile([P, P], F32)
         nsel = keep.tile([P, 4, P], BF16)
+        negr = keep.tile([P, P, 4], BF16)
         b_sb = keep.tile([P, 8, 1024], BF16)
         tr1 = keep.tile([P, 4, 512], BF16)
         tr2 = keep.tile([P, 4, 256], BF16)
@@ -107,15 +108,16 @@ def tile_mex_t_kernel(tc, x, offsets, out):
             )
 
         def transpose_pooled(hh):
-            pt = bank(3, [P, 4, P], BF16)
+            pt = bank(3, [P, 5, P], BF16)
             for jj in range(4):
                 nc.tensor.transpose(pt[:, jj, :], p4[:, hh, jj * P : (jj + 1) * P], ident[:])
+            nc.tensor.transpose(pt[:, 4, :], p4[:, hh, :].rearrange("p (q bb) -> p q bb", bb=4)[:, :, 0], ident[:])
             return pt
 
         def max_over_channels(hh, pt):
             with nc.allow_low_precision(reason="a maximum of bfloat16 values is a bfloat16 value"):
                 nc.vector.tensor_reduce(
-                    out=mt_col[:, hh, 0:16],
+                    out=mt_col[:, hh, 0:20],
                     in_=pt[:].rearrange("p j (i c) -> p (j i) c", c=32),
                     axis=AX.X,
                     op=ALU.max,
@@ -155,7 +157,15 @@ def tile_mex_t_kernel(tc, x, offsets, out):
                 start=True,
                 stop=False,
             )
-            for jj in range(4):
+            if b == 0:
+                nc.tensor.matmul(
+                    out=dps[:],
+                    lhsT=mt_col[:, hh, 16 + i : 17 + i].to_broadcast([P, P]),
+                    rhs=negr[:].rearrange("p q d -> p (q d)"),
+                    start=False,
+                    stop=True,
+                )
+            for jj in range(4 if b > 0 else 0):
                 k = 4 * jj + i
                 nc.tensor.matmul(
                     out=dps[:, jj * P : (jj + 1) * P],
@@ -167,27 +177,14 @@ def tile_mex_t_kernel(tc, x, offsets, out):
                 )
             nc.scalar.activation(out=e_tile[:, g, b * 512 : (b + 1) * 512], in_=dps[:], func=ACT.Exp)
 
-        def subtract_on_vector(i, hh, g, b, dst):
-            nc.vector.tensor_tensor(
-                out=dst.rearrange("p (hl a d) -> p hl a d", a=8, d=4),
-                in0=xs[:, g, i, :]
-                .rearrange("p (h w) -> p h w", w=35)[:, 16 * hh : 16 * hh + 16, b : b + 32]
-                .rearrange("p hl (a d) -> p hl a d", d=4),
-                in1=mxp[i][:, hh * 512 : (hh + 1) * 512]
-                .rearrange("p (hl a bb) -> p hl a bb", a=8, bb=4)[:, :, :, b]
-                .unsqueeze(3)
-                .to_broadcast([P, 16, 8, 4]),
-                op=ALU.subtract,
-            )
-
-        def subtract_on_gpsimd(i, hh, d_tile):
-            nc.gpsimd.tensor_tensor(
-                out=d_tile[:, 1:3, :].rearrange("p g (hl a d) -> p g hl a d", a=8, d=4),
+        def subtract(eng, m_ap, i, hh, b, d_tile):
+            eng.tensor_tensor(
+                out=d_tile[:, :, b - 2, :].rearrange("p g (hl a d) -> p g hl a d", a=8, d=4),
                 in0=xs[:, :, i, :]
-                .rearrange("p g (h w) -> p g h w", w=35)[:, :, 16 * hh : 16 * hh + 16, 3:35]
+                .rearrange("p g (h w) -> p g h w", w=35)[:, :, 16 * hh : 16 * hh + 16, b : b + 32]
                 .rearrange("p g hl (a d) -> p g hl a d", d=4),
-                in1=mxs[:, i, hh * 512 : (hh + 1) * 512]
-                .rearrange("p (hl a bb) -> p hl a bb", a=8, bb=4)[:, :, :, 3]
+                in1=m_ap[:, hh * 512 : (hh + 1) * 512]
+                .rearrange("p (hl a bb) -> p hl a bb", a=8, bb=4)[:, :, :, b]
                 .unsqueeze(1)
                 .unsqueeze(4)
                 .to_broadcast([P, 2, 16, 8, 4]),
@@ -195,12 +192,9 @@ def tile_mex_t_kernel(tc, x, offsets, out):
             )
 
         def exp_piece(g, d_tile, e_tile):
-            if g == 0:
-                nc.scalar.activation(
-                    out=e_tile[:, 0, 1024:2048], in_=d_tile[:, 0:2, :].rearrange("p b n -> p (b n)"), func=ACT.Exp
-                )
-            else:
-                nc.scalar.activation(out=e_tile[:, 1, 1536:2048], in_=d_tile[:, 2, :], func=ACT.Exp)
+            nc.scalar.activation(
+                out=e_tile[:, g, 1024:2048], in_=d_tile[:, g].rearrange("p b n -> p (b n)"), func=ACT.Exp
+            )
 
         def quantise_ex(hh, i, e_tile):
             nc.vector.quantize_mx(
@@ -232,6 +226,7 @@ def tile_mex_t_kernel(tc, x, offsets, out):
         make_identity(nc, ident[:])
         nc.vector.memset(mt_col[:], 0.0)
         nc.vector.tensor_copy(out=ident32[:], in_=ident[:])
+        nc.vector.tensor_scalar_mul(out=negr[:], in0=ident[:].unsqueeze(2).to_broadcast([P, P, 4]), scalar1=-1.0)
         for b in range(4):
             nc.vector.tensor_scalar_mul(
                 out=nsel[:, b, :].rearrange("p (r a d) -> p r a d", a=8, d=4),
@@ -278,12 +273,12 @@ def tile_mex_t_kernel(tc, x, offsets, out):
 
         def prepare_g(u):
             hh, i = units[u]
-            d_tiles[u] = dpool.tile([P, 3, 512], F32, name="dt")
-            subtract_on_gpsimd(i, hh, d_tiles[u])
+            d_tiles[u] = dpool.tile([P, 2, 2, 512], F32, name="dt")
+            subtract(nc.gpsimd, mxs[:, i, :], i, hh, 3, d_tiles[u])
 
         def prepare_v(u):
             hh, i = units[u]
-            subtract_on_vector(i, hh, 0, 2, d_tiles[u][:, 0, :])
+            subtract(nc.vector, mxp[i], i, hh, 2, d_tiles[u])
 
         def chunks(u, todo):
             hh, i = units[u]
@@ -302,16 +297,15 @@ def tile_mex_t_kernel(tc, x, offsets, out):
         spread_mx(0, 1)
         copy_mx(0, 1)
         prepare_g(1)
-        d_tiles[0] = dpool.tile([P, 3, 512], F32, name="dt")
-        subtract_on_vector(0, 0, 0, 2, d_tiles[0][:, 0, :])
-        subtract_on_vector(0, 0, 0, 3, d_tiles[0][:, 1, :])
-        subtract_on_vector(0, 0, 1, 3, d_tiles[0][:, 2, :])
+        d_tiles[0] = dpool.tile([P, 2, 2, 512], F32, name="dt")
+        subtract(nc.vector, mxp[0], 0, 0, 2, d_tiles[0])
+        subtract(nc.vector, mxp[0], 0, 0, 3, d_tiles[0])
         for u in range(8):
             hh, i = units[u]
             e_tiles[u] = epool.tile([P, 2, 2048], BF16, name="et_ex", align_bytes=64)
             chunks(u, [(0, 0), (0, 1)])
             if u == 0:
-                chunks(u, [(1, 0), (1, 1), (1, 2)])
+                chunks(u, [(1, 0), (1, 1)])
                 spread_mx(0, 2)
                 spread_mx(0, 3)
                 copy_mx(0, 2)
@@ -324,12 +318,9 @@ def tile_mex_t_kernel(tc, x, offsets, out):
                 pool_b(1)
             else:
                 exp_piece(0, d_tiles[u], e_tiles[u])
-                if u == 2:
-                    sp1 = select_negated(1)
-                    copy_negated(1, sp1)
                 if u == 7:
                     eb_codes(6)
-                chunks(u, [(1, 0), (1, 1), (1, 2)])
+                chunks(u, [(1, 0), (1, 1)])
                 if u == 1:
                     prepare_v(2)
                     prepare_v(3)
@@ -339,6 +330,9 @@ def tile_mex_t_kernel(tc, x, offsets, out):
             if u == 1:
                 pt1 = transpose_pooled(1)
                 max_over_channels(1, pt1)
+            if u == 2:
+                sp1 = select_negated(1)
+                copy_negated(1, sp1)
             if u == 2 or u == 3:
                 for v in (2 * u - 4, 2 * u - 3):
                     spread_mx(1, v)

@@ -25,7 +25,8 @@ def tile_mex_t_kernel(tc, x, offsets, out):
         dpool = ctx.enter_context(tc.tile_pool(name="dpool", bufs=4))
         epool = ctx.enter_context(tc.tile_pool(name="epool", bufs=3))
         gpool = ctx.enter_context(tc.tile_pool(name="gpool", bufs=2))
-        opool = ctx.enter_context(tc.tile_pool(name="opool", bufs=8))
+        opool = ctx.enter_context(tc.tile_pool(name="opool", bufs=6))
+        qpool = ctx.enter_context(tc.tile_pool(name="qpool", bufs=3))
         ps = ctx.enter_context(tc.psum_pool(name="ps", bufs=1))
         ctx.enter_context(tc.manual_schedule())
 
@@ -67,15 +68,12 @@ def tile_mex_t_kernel(tc, x, offsets, out):
         def bank(k, shape, dtype):
             return ps.tile(shape, dtype, tag="bank%d" % k, name="bk%d" % k)
 
-        def load_x_rows(pr):
-            for g in range(2):
-                for dh in range(4):
-                    nc.sync.dma_start(
-                        out=xs[dh:P:4, g, 2 * pr : 2 * pr + 2, :],
-                        in_=x[2 * pr : 2 * pr + 2, 32 * g : 32 * g + 32, dh : dh + 32, :].rearrange(
-                            "i c h w -> c i (h w)"
-                        ),
-                    )
+        def load_x_rows(hh, i):
+            for dh in range(4):
+                nc.sync.dma_start(
+                    out=xs[dh:P:4, :, i, 560 * hh : 560 * hh + 560],
+                    in_=x[i, :, dh + 16 * hh : dh + 16 * hh + 16, :].rearrange("(g c) h w -> c g (h w)", g=2),
+                )
 
         def max_of_b(m0, n):
             s = slice(m0, m0 + n)
@@ -243,8 +241,9 @@ def tile_mex_t_kernel(tc, x, offsets, out):
         nc.sync.dma_start(out=xq[:], in_=xq_v)
         nc.sync.dma_start(out=b_sb[:, 4:6, :], in_=bv[:, 4:6, :])
         nc.sync.dma_start(out=b_sb[:, 6:8, :], in_=bv[:, 6:8, :])
-        load_x_rows(0)
-        load_x_rows(1)
+        for hh in range(2):
+            for i in range(4):
+                load_x_rows(hh, i)
 
         max_of_b(0, 1)
         exp_of_b(0)
@@ -314,6 +313,7 @@ def tile_mex_t_kernel(tc, x, offsets, out):
                 prepare_g(3)
                 prepare_v(1)
                 exp_piece(0, d_tiles[u], e_tiles[u])
+                copy_mx(0, 0)
                 pool_a(1)
                 pool_b(1)
             else:
@@ -350,37 +350,61 @@ def tile_mex_t_kernel(tc, x, offsets, out):
         )
 
         acc_no = [0]
+
+        def sums(i, mt, hh):
+            acc = bank(acc_no[0] % 4, [P, 512], F32)
+            acc_no[0] += 1
+            for g in range(2):
+                nc.tensor.matmul_mx(
+                    out=acc[:],
+                    lhsT=ebc[:, g, mt * P : (mt + 1) * P].bitcast(FP8X4),
+                    lhsT_scale=ebs[:, g, mt * P : (mt + 1) * P],
+                    rhs=exc[:, 2 * i + hh, g, :].bitcast(FP8X4),
+                    rhs_scale=exs[:, 2 * i + hh, g, :],
+                    start=(g == 0),
+                    stop=(g == 1),
+                )
+            return acc
+
+        def log_of(acc, ot, hh, r0, nr):
+            c0 = hh * 512 + r0 * 32
+            nc.scalar.activation(
+                out=ot[:, c0 : c0 + nr * 32].rearrange("p (hl a bb) -> p hl a bb", a=8, bb=4),
+                in_=acc[:].rearrange("p (bb hl a) -> p hl a bb", bb=4, a=8)[:, r0 : r0 + nr],
+                func=ACT.Ln,
+            )
+
+        def finish(i, mt, ot, c0, n):
+            s = slice(c0, c0 + n)
+            nc.vector.scalar_tensor_tensor(
+                out=ot[:, s], in0=ot[:, s], scalar=mbc[:, mt : mt + 1], in1=mxp[i][:, s], op0=ALU.add, op1=ALU.add
+            )
+            nc.sync.dma_start(out=ov[i][:, mt, s], in_=ot[:, s])
+
+        late = []
         for i in range(4):
             for mt in range(8):
-                ot = opool.tile([P, 1024], F32, name="ot")
-                last = i == 3 and mt == 7
+                if late and late[0][0] == 8 * i + mt:
+                    nc.sync.dma_start(out=ov[late[0][1]][:, late[0][2], :], in_=late[0][3][:])
+                    late.pop(0)
+                on_gpsimd = mt % 4 == 1 and 8 * i + mt < 22
+                if on_gpsimd:
+                    ot = qpool.tile([P, 1024], F32, name="oq")
+                else:
+                    ot = opool.tile([P, 1024], F32, name="ot")
+                if i == 3 and mt == 7:
+                    log_of(sums(i, mt, 0), ot, 0, 0, 16)
+                    finish(i, mt, ot, 0, 512)
+                    log_of(sums(i, mt, 1), ot, 1, 0, 16)
+                    finish(i, mt, ot, 512, 512)
+                    continue
                 for hh in range(2):
-                    acc = bank(acc_no[0] % 4, [P, 512], F32)
-                    acc_no[0] += 1
-                    for g in range(2):
-                        nc.tensor.matmul_mx(
-                            out=acc[:],
-                            lhsT=ebc[:, g, mt * P : (mt + 1) * P].bitcast(FP8X4),
-                            lhsT_scale=ebs[:, g, mt * P : (mt + 1) * P],
-                            rhs=exc[:, 2 * i + hh, g, :].bitcast(FP8X4),
-                            rhs_scale=exs[:, 2 * i + hh, g, :],
-                            start=(g == 0),
-                            stop=(g == 1),
-                        )
-                    nc.scalar.activation(
-                        out=ot[:, hh * 512 : (hh + 1) * 512].rearrange("p (hl a bb) -> p hl a bb", a=8, bb=4),
-                        in_=acc[:].rearrange("p (bb hl a) -> p hl a bb", bb=4, a=8),
-                        func=ACT.Ln,
+                    log_of(sums(i, mt, hh), ot, hh, 0, 16)
+                if on_gpsimd:
+                    nc.gpsimd.tensor_tensor(out=ot[:], in0=ot[:], in1=mxs[:, i, :], op=ALU.add)
+                    nc.gpsimd.tensor_scalar(
+                        out=ot[:], in0=ot[:], scalar1=1.0, scalar2=mbc[:, mt : mt + 1], op0=ALU.mult, op1=ALU.add
                     )
-                    if last:
-                        s = slice(hh * 512, (hh + 1) * 512)
-                        nc.vector.scalar_tensor_tensor(
-                            out=ot[:, s], in0=ot[:, s], scalar=mbc[:, mt : mt + 1], in1=mxp[i][:, s],
-                            op0=ALU.add, op1=ALU.add,
-                        )
-                        nc.sync.dma_start(out=ov[i][:, mt, s], in_=ot[:, s])
-                if not last:
-                    nc.vector.scalar_tensor_tensor(
-                        out=ot[:], in0=ot[:], scalar=mbc[:, mt : mt + 1], in1=mxp[i][:], op0=ALU.add, op1=ALU.add
-                    )
-                    nc.sync.dma_start(out=ov[i][:, mt, :], in_=ot[:])
+                    late.append((8 * i + mt + 3, i, mt, ot))
+                else:
+                    finish(i, mt, ot, 0, 1024)

@@ -25,8 +25,7 @@ def tile_mex_t_kernel(tc, x, offsets, out):
         dpool = ctx.enter_context(tc.tile_pool(name="dpool", bufs=4))
         epool = ctx.enter_context(tc.tile_pool(name="epool", bufs=3))
         gpool = ctx.enter_context(tc.tile_pool(name="gpool", bufs=2))
-        opool = ctx.enter_context(tc.tile_pool(name="opool", bufs=6))
-        qpool = ctx.enter_context(tc.tile_pool(name="qpool", bufs=3))
+        opool = ctx.enter_context(tc.tile_pool(name="opool", bufs=8))
         ps = ctx.enter_context(tc.psum_pool(name="ps", bufs=1))
         ctx.enter_context(tc.manual_schedule())
 
@@ -59,21 +58,24 @@ def tile_mex_t_kernel(tc, x, offsets, out):
         xs = keep.tile([P, 2, 4, 1120], BF16)
         exc = keep.tile([P, 8, 2, 512], U32, align_bytes=64)
         exs = keep.tile([P, 8, 2, 512], U8, align_bytes=64)
-        mxp0 = ps.tile([P, 1024], BF16)
-        mxp1 = ps.tile([P, 1024], BF16)
-        mxp2 = ps.tile([P, 1024], BF16)
-        mxp3 = ps.tile([P, 1024], BF16)
+        mxp0 = ps.tile([P, 1024], BF16, tag="mxp0", name="mxp0")
+        mxp1 = ps.tile([P, 1024], BF16, tag="mxp1", name="mxp1")
+        mxp2 = ps.tile([P, 1024], BF16, tag="mxp2", name="mxp2")
+        mxp3 = ps.tile([P, 1024], BF16, tag="mxp3", name="mxp3")
         mxp = [mxp0, mxp1, mxp2, mxp3]
 
         def bank(k, shape, dtype):
             return ps.tile(shape, dtype, tag="bank%d" % k, name="bk%d" % k)
 
-        def load_x_rows(hh, i):
-            for dh in range(4):
-                nc.sync.dma_start(
-                    out=xs[dh:P:4, :, i, 560 * hh : 560 * hh + 560],
-                    in_=x[i, :, dh + 16 * hh : dh + 16 * hh + 16, :].rearrange("(g c) h w -> c g (h w)", g=2),
-                )
+        def load_x_rows(pr):
+            for g in range(2):
+                for dh in range(4):
+                    nc.sync.dma_start(
+                        out=xs[dh:P:4, g, 2 * pr : 2 * pr + 2, :],
+                        in_=x[2 * pr : 2 * pr + 2, 32 * g : 32 * g + 32, dh : dh + 32, :].rearrange(
+                            "i c h w -> c i (h w)"
+                        ),
+                    )
 
         def max_of_b(m0, n):
             s = slice(m0, m0 + n)
@@ -241,9 +243,8 @@ def tile_mex_t_kernel(tc, x, offsets, out):
         nc.sync.dma_start(out=xq[:], in_=xq_v)
         nc.sync.dma_start(out=b_sb[:, 4:6, :], in_=bv[:, 4:6, :])
         nc.sync.dma_start(out=b_sb[:, 6:8, :], in_=bv[:, 6:8, :])
-        for hh in range(2):
-            for i in range(4):
-                load_x_rows(hh, i)
+        load_x_rows(0)
+        load_x_rows(1)
 
         max_of_b(0, 1)
         exp_of_b(0)
@@ -350,61 +351,41 @@ def tile_mex_t_kernel(tc, x, offsets, out):
         )
 
         acc_no = [0]
-
-        def sums(i, mt, hh):
-            acc = bank(acc_no[0] % 4, [P, 512], F32)
-            acc_no[0] += 1
-            for g in range(2):
-                nc.tensor.matmul_mx(
-                    out=acc[:],
-                    lhsT=ebc[:, g, mt * P : (mt + 1) * P].bitcast(FP8X4),
-                    lhsT_scale=ebs[:, g, mt * P : (mt + 1) * P],
-                    rhs=exc[:, 2 * i + hh, g, :].bitcast(FP8X4),
-                    rhs_scale=exs[:, 2 * i + hh, g, :],
-                    start=(g == 0),
-                    stop=(g == 1),
-                )
-            return acc
-
-        def log_of(acc, ot, hh, r0, nr):
-            c0 = hh * 512 + r0 * 32
-            nc.scalar.activation(
-                out=ot[:, c0 : c0 + nr * 32].rearrange("p (hl a bb) -> p hl a bb", a=8, bb=4),
-                in_=acc[:].rearrange("p (bb hl a) -> p hl a bb", bb=4, a=8)[:, r0 : r0 + nr],
-                func=ACT.Ln,
-            )
-
-        def finish(i, mt, ot, c0, n):
-            s = slice(c0, c0 + n)
-            nc.vector.scalar_tensor_tensor(
-                out=ot[:, s], in0=ot[:, s], scalar=mbc[:, mt : mt + 1], in1=mxp[i][:, s], op0=ALU.add, op1=ALU.add
-            )
-            nc.sync.dma_start(out=ov[i][:, mt, s], in_=ot[:, s])
-
-        late = []
         for i in range(4):
             for mt in range(8):
-                if late and late[0][0] == 8 * i + mt:
-                    nc.sync.dma_start(out=ov[late[0][1]][:, late[0][2], :], in_=late[0][3][:])
-                    late.pop(0)
-                on_gpsimd = mt % 4 == 1 and 8 * i + mt < 22
-                if on_gpsimd:
-                    ot = qpool.tile([P, 1024], F32, name="oq")
-                else:
-                    ot = opool.tile([P, 1024], F32, name="ot")
-                if i == 3 and mt == 7:
-                    log_of(sums(i, mt, 0), ot, 0, 0, 16)
-                    finish(i, mt, ot, 0, 512)
-                    log_of(sums(i, mt, 1), ot, 1, 0, 16)
-                    finish(i, mt, ot, 512, 512)
-                    continue
+                ot = opool.tile([P, 1024], F32, name="ot")
+                last = i == 3 and mt == 7
                 for hh in range(2):
-                    log_of(sums(i, mt, hh), ot, hh, 0, 16)
-                if on_gpsimd:
-                    nc.gpsimd.tensor_tensor(out=ot[:], in0=ot[:], in1=mxs[:, i, :], op=ALU.add)
-                    nc.gpsimd.tensor_scalar(
-                        out=ot[:], in0=ot[:], scalar1=1.0, scalar2=mbc[:, mt : mt + 1], op0=ALU.mult, op1=ALU.add
+                    k = acc_no[0] % 8
+                    acc_no[0] += 1
+                    if k < 4:
+                        acc = bank(k, [P, 512], F32)
+                    else:
+                        acc = ps.tile([P, 512], F32, tag="mxp%d" % (k - 4), name="ac%d" % k)
+                    for g in range(2):
+                        nc.tensor.matmul_mx(
+                            out=acc[:],
+                            lhsT=ebc[:, g, mt * P : (mt + 1) * P].bitcast(FP8X4),
+                            lhsT_scale=ebs[:, g, mt * P : (mt + 1) * P],
+                            rhs=exc[:, 2 * i + hh, g, :].bitcast(FP8X4),
+                            rhs_scale=exs[:, 2 * i + hh, g, :],
+                            start=(g == 0),
+                            stop=(g == 1),
+                        )
+                    nc.scalar.activation(
+                        out=ot[:, hh * 512 : (hh + 1) * 512].rearrange("p (hl a bb) -> p hl a bb", a=8, bb=4),
+                        in_=acc[:].rearrange("p (bb hl a) -> p hl a bb", bb=4, a=8),
+                        func=ACT.Ln,
                     )
-                    late.append((8 * i + mt + 3, i, mt, ot))
-                else:
-                    finish(i, mt, ot, 0, 1024)
+                    if last:
+                        s = slice(hh * 512, (hh + 1) * 512)
+                        nc.vector.scalar_tensor_tensor(
+                            out=ot[:, s], in0=ot[:, s], scalar=mbc[:, mt : mt + 1], in1=mxs[:, i, s],
+                            op0=ALU.add, op1=ALU.add,
+                        )
+                        nc.sync.dma_start(out=ov[i][:, mt, s], in_=ot[:, s])
+                if not last:
+                    nc.vector.scalar_tensor_tensor(
+                        out=ot[:], in0=ot[:], scalar=mbc[:, mt : mt + 1], in1=mxs[:, i, :], op0=ALU.add, op1=ALU.add
+                    )
+                    nc.sync.dma_start(out=ov[i][:, mt, :], in_=ot[:])

@@ -86,8 +86,8 @@ def tile_mex_t_kernel(tc, x, offsets, out):
 
         def exp_of_b(mt):
             nc.scalar.activation(
-                out=ebp[:, mt, :].rearrange("m (g t p) -> m g t p", g=2, t=4),
-                in_=b_sb[:, mt, :].rearrange("m (g p t) -> m g t p", g=2, t=4),
+                out=ebp[:, mt, :],
+                in_=b_sb[:, mt, :],
                 func=ACT.Exp,
                 bias=nmb[:, mt : mt + 1],
                 scale=1.0,
@@ -191,6 +191,20 @@ def tile_mex_t_kernel(tc, x, offsets, out):
                 op=ALU.subtract,
             )
 
+        def subtract_part(eng, m_ap, i, hh, b, d_tile, g, q):
+            h0 = 16 * hh + 8 * q
+            eng.tensor_tensor(
+                out=d_tile[:, g, b - 2, 256 * q : 256 * q + 256].rearrange("p (hl a d) -> p hl a d", a=8, d=4),
+                in0=xs[:, g, i, :]
+                .rearrange("p (h w) -> p h w", w=35)[:, h0 : h0 + 8, b : b + 32]
+                .rearrange("p hl (a d) -> p hl a d", d=4),
+                in1=m_ap[:, h0 * 32 : h0 * 32 + 256]
+                .rearrange("p (hl a bb) -> p hl a bb", a=8, bb=4)[:, :, :, b]
+                .unsqueeze(3)
+                .to_broadcast([P, 8, 8, 4]),
+                op=ALU.subtract,
+            )
+
         def exp_piece(g, d_tile, e_tile):
             nc.scalar.activation(
                 out=e_tile[:, g, 1024:2048], in_=d_tile[:, g].rearrange("p b n -> p (b n)"), func=ACT.Exp
@@ -204,15 +218,17 @@ def tile_mex_t_kernel(tc, x, offsets, out):
             )
 
         def transpose_eb(mt):
-            et = bank(3, [P, 8, P], BF16)
-            for gt in range(8):
-                nc.tensor.transpose(et[:, gt, :], ebp[:, mt, gt * P : (gt + 1) * P], ident[:])
+            et = bank(3, [P, 4, P], F32)
+            words = ebp[:, mt, :].bitcast(F32)
+            for g in range(2):
+                for v in range(2):
+                    nc.tensor.transpose(et[:, 2 * g + v, :], words[:, 256 * g + v : 256 * (g + 1) : 2], ident32[:])
             return et
 
         def regroup_eb(mt, et, ebg):
             ml = mt % 2
             nc.vector.tensor_copy(
-                out=ebg[:, :, ml * P : (ml + 1) * P, :], in_=et[:].rearrange("p (g t) m -> p g m t", g=2)
+                out=ebg[:, :, ml * P : (ml + 1) * P, :], in_=et[:].rearrange("p (g v) m -> p g m v", g=2)
             )
 
         def quantise_eb(mp, ebg):
@@ -220,7 +236,7 @@ def tile_mex_t_kernel(tc, x, offsets, out):
                 nc.vector.quantize_mx(
                     out=ebc[:, g, mp * 256 : (mp + 1) * 256].bitcast(FP8X4),
                     scales=ebs[:, g, mp * 256 : (mp + 1) * 256],
-                    in_=ebg[:, g].rearrange("p m t -> p (m t)"),
+                    in_=ebg[:, g].rearrange("p m v -> p (m v)").bitcast(BF16),
                 )
 
         make_identity(nc, ident[:])
@@ -274,7 +290,9 @@ def tile_mex_t_kernel(tc, x, offsets, out):
         def prepare_g(u):
             hh, i = units[u]
             d_tiles[u] = dpool.tile([P, 2, 2, 512], F32, name="dt")
-            subtract(nc.gpsimd, mxs[:, i, :], i, hh, 3, d_tiles[u])
+            for g in range(2):
+                for q in range(2):
+                    subtract_part(nc.gpsimd, mxs[:, i, :], i, hh, 3, d_tiles[u], g, q)
 
         def prepare_v(u):
             hh, i = units[u]
@@ -288,7 +306,7 @@ def tile_mex_t_kernel(tc, x, offsets, out):
         def eb_codes(mt):
             et = transpose_eb(mt)
             if mt % 2 == 0:
-                ebg_now[0] = gpool.tile([P, 2, 256, 4], BF16, name="ebg", align_bytes=64)
+                ebg_now[0] = gpool.tile([P, 2, 256, 2], F32, name="ebg", align_bytes=64)
             regroup_eb(mt, et, ebg_now[0])
             if mt % 2 == 1:
                 quantise_eb(mt // 2, ebg_now[0])

@@ -58,11 +58,10 @@ def tile_mex_t_kernel(tc, x, offsets, out):
         xs = keep.tile([P, 2, 4, 1120], BF16)
         exc = keep.tile([P, 8, 2, 512], U32, align_bytes=64)
         exs = keep.tile([P, 8, 2, 512], U8, align_bytes=64)
-        mxp0 = ps.tile([P, 1024], BF16, tag="mxp0", name="mxp0")
-        mxp1 = ps.tile([P, 1024], BF16, tag="mxp1", name="mxp1")
-        mxp2 = ps.tile([P, 1024], BF16, tag="mxp2", name="mxp2")
-        mxp3 = ps.tile([P, 1024], BF16, tag="mxp3", name="mxp3")
-        mxp = [mxp0, mxp1, mxp2, mxp3]
+        CHUNK_BANKS = 5
+        SIDE_BANK = 5
+        MX_BANK = 6
+        mxp = [None, None]
 
         def bank(k, shape, dtype):
             return ps.tile(shape, dtype, tag="bank%d" % k, name="bk%d" % k)
@@ -108,7 +107,7 @@ def tile_mex_t_kernel(tc, x, offsets, out):
             )
 
         def transpose_pooled(hh):
-            pt = bank(3, [P, 5, P], BF16)
+            pt = bank(SIDE_BANK, [P, 5, P], BF16)
             for jj in range(4):
                 nc.tensor.transpose(pt[:, jj, :], p4[:, hh, jj * P : (jj + 1) * P], ident[:])
             nc.tensor.transpose(pt[:, 4, :], p4[:, hh, :].rearrange("p (q bb) -> p q bb", bb=4)[:, :, 0], ident[:])
@@ -124,7 +123,7 @@ def tile_mex_t_kernel(tc, x, offsets, out):
                 )
 
         def select_negated(hh):
-            selp = bank(3, [P, 4, 32], F32)
+            selp = bank(SIDE_BANK, [P, 4, 32], F32)
             for b in range(4):
                 nc.tensor.matmul(out=selp[:, b, :], lhsT=nsel[:, b, :], rhs=mt_col[:, hh, :], start=True, stop=True)
             return selp
@@ -132,50 +131,62 @@ def tile_mex_t_kernel(tc, x, offsets, out):
         def copy_negated(hh, selp):
             nc.vector.tensor_copy(out=negm[:, hh], in_=selp[:])
 
-        def spread_mx(hh, i):
-            for jj in range(4):
-                k = 4 * jj + i
-                j = 4 * hh + jj
-                nc.tensor.transpose(
-                    mxp[i][:, j * P : (j + 1) * P], mt_col[:, hh, k : k + 1].to_broadcast([P, P]), ident[:]
-                )
+        def spread_mx(hh, pr):
+            mxp[pr] = bank(MX_BANK + pr, [P, 2, 512], BF16)
+            for il in range(2):
+                for jj in range(4):
+                    k = 4 * jj + 2 * pr + il
+                    nc.tensor.transpose(
+                        mxp[pr][:, il, jj * P : (jj + 1) * P], mt_col[:, hh, k : k + 1].to_broadcast([P, P]), ident[:]
+                    )
 
-        def copy_mx(hh, i):
-            s = slice(hh * 512, (hh + 1) * 512)
-            nc.vector.tensor_copy(out=mxs[:, i, s], in_=mxp[i][:, s])
+        def copy_mx(hh, pr):
+            nc.vector.tensor_copy(out=mxs[:, 2 * pr : 2 * pr + 2, hh * 512 : (hh + 1) * 512], in_=mxp[pr][:])
 
         chunk_no = [0]
 
-        def chunk_on_pe(g, i, hh, b, e_tile):
-            dps = bank(chunk_no[0] % 3, [P, 512], F32)
-            chunk_no[0] += 1
+        def chunk_pair(g, i, hh, e_tile):
+            dps = []
+            for b in range(2):
+                dps.append(bank(chunk_no[0] % CHUNK_BANKS, [P, 512], F32))
+                chunk_no[0] += 1
             rows = xs[:, g, i, :].rearrange("p (h w) -> p h w", w=35)
-            nc.tensor.matmul(
-                out=dps[:].rearrange("p (r w) -> p r w", w=32),
-                lhsT=ident[:],
-                rhs=rows[:, 16 * hh : 16 * hh + 16, b : b + 32],
-                start=True,
-                stop=False,
-            )
-            if b == 0:
+
+            def copy_x(b):
                 nc.tensor.matmul(
-                    out=dps[:],
-                    lhsT=mt_col[:, hh, 16 + i : 17 + i].to_broadcast([P, P]),
-                    rhs=negr[:].rearrange("p q d -> p (q d)"),
-                    start=False,
-                    stop=True,
+                    out=dps[b][:].rearrange("p (r w) -> p r w", w=32),
+                    lhsT=ident[:],
+                    rhs=rows[:, 16 * hh : 16 * hh + 16, b : b + 32],
+                    start=True,
+                    stop=False,
                 )
-            for jj in range(4 if b > 0 else 0):
+
+            def add_quarter(jj):
                 k = 4 * jj + i
                 nc.tensor.matmul(
-                    out=dps[:, jj * P : (jj + 1) * P],
-                    lhsT=negm[:, hh, b, k : k + 1].to_broadcast([P, P]),
+                    out=dps[1][:, jj * P : (jj + 1) * P],
+                    lhsT=negm[:, hh, 1, k : k + 1].to_broadcast([P, P]),
                     rhs=ident32[:],
                     is_transpose=True,
                     start=False,
                     stop=(jj == 3),
                 )
-            nc.scalar.activation(out=e_tile[:, g, b * 512 : (b + 1) * 512], in_=dps[:], func=ACT.Exp)
+
+            copy_x(1)
+            add_quarter(0)
+            copy_x(0)
+            add_quarter(1)
+            nc.tensor.matmul(
+                out=dps[0][:],
+                lhsT=mt_col[:, hh, 16 + i : 17 + i].to_broadcast([P, P]),
+                rhs=negr[:].rearrange("p q d -> p (q d)"),
+                start=False,
+                stop=True,
+            )
+            add_quarter(2)
+            add_quarter(3)
+            for b in range(2):
+                nc.scalar.activation(out=e_tile[:, g, b * 512 : (b + 1) * 512], in_=dps[b][:], func=ACT.Exp)
 
         def subtract(eng, m_ap, i, hh, b, d_tile):
             eng.tensor_tensor(
@@ -183,7 +194,7 @@ def tile_mex_t_kernel(tc, x, offsets, out):
                 in0=xs[:, :, i, :]
                 .rearrange("p g (h w) -> p g h w", w=35)[:, :, 16 * hh : 16 * hh + 16, b : b + 32]
                 .rearrange("p g hl (a d) -> p g hl a d", d=4),
-                in1=m_ap[:, hh * 512 : (hh + 1) * 512]
+                in1=m_ap
                 .rearrange("p (hl a bb) -> p hl a bb", a=8, bb=4)[:, :, :, b]
                 .unsqueeze(1)
                 .unsqueeze(4)
@@ -198,7 +209,7 @@ def tile_mex_t_kernel(tc, x, offsets, out):
                 in0=xs[:, g, i, :]
                 .rearrange("p (h w) -> p h w", w=35)[:, h0 : h0 + 8, b : b + 32]
                 .rearrange("p hl (a d) -> p hl a d", d=4),
-                in1=m_ap[:, h0 * 32 : h0 * 32 + 256]
+                in1=m_ap[:, 256 * q : 256 * q + 256]
                 .rearrange("p (hl a bb) -> p hl a bb", a=8, bb=4)[:, :, :, b]
                 .unsqueeze(3)
                 .to_broadcast([P, 8, 8, 4]),
@@ -218,7 +229,7 @@ def tile_mex_t_kernel(tc, x, offsets, out):
             )
 
         def transpose_eb(mt):
-            et = bank(3, [P, 4, P], F32)
+            et = bank(SIDE_BANK, [P, 4, P], F32)
             words = ebp[:, mt, :].bitcast(F32)
             for g in range(2):
                 for v in range(2):
@@ -287,21 +298,28 @@ def tile_mex_t_kernel(tc, x, offsets, out):
         e_tiles = {}
         ebg_now = [None]
 
+        def mx_sbuf(u):
+            hh, i = units[u]
+            return mxs[:, i, hh * 512 : (hh + 1) * 512]
+
+        def mx_psum(u):
+            hh, i = units[u]
+            return mxp[i // 2][:, i % 2, :]
+
         def prepare_g(u):
             hh, i = units[u]
             d_tiles[u] = dpool.tile([P, 2, 2, 512], F32, name="dt")
             for g in range(2):
                 for q in range(2):
-                    subtract_part(nc.gpsimd, mxs[:, i, :], i, hh, 3, d_tiles[u], g, q)
+                    subtract_part(nc.gpsimd, mx_sbuf(u), i, hh, 3, d_tiles[u], g, q)
 
         def prepare_v(u):
             hh, i = units[u]
-            subtract(nc.vector, mxp[i], i, hh, 2, d_tiles[u])
+            subtract(nc.vector, mx_psum(u), i, hh, 2, d_tiles[u])
 
-        def chunks(u, todo):
+        def chunks(u, g):
             hh, i = units[u]
-            for g, b in todo:
-                chunk_on_pe(g, i, hh, b, e_tiles[u])
+            chunk_pair(g, i, hh, e_tiles[u])
 
         def eb_codes(mt):
             et = transpose_eb(mt)
@@ -312,34 +330,30 @@ def tile_mex_t_kernel(tc, x, offsets, out):
                 quantise_eb(mt // 2, ebg_now[0])
 
         spread_mx(0, 0)
-        spread_mx(0, 1)
-        copy_mx(0, 1)
+        copy_mx(0, 0)
         prepare_g(1)
         d_tiles[0] = dpool.tile([P, 2, 2, 512], F32, name="dt")
-        subtract(nc.vector, mxp[0], 0, 0, 2, d_tiles[0])
-        subtract(nc.vector, mxp[0], 0, 0, 3, d_tiles[0])
+        subtract(nc.vector, mx_psum(0), 0, 0, 2, d_tiles[0])
+        subtract(nc.vector, mx_psum(0), 0, 0, 3, d_tiles[0])
         for u in range(8):
             hh, i = units[u]
             e_tiles[u] = epool.tile([P, 2, 2048], BF16, name="et_ex", align_bytes=64)
-            chunks(u, [(0, 0), (0, 1)])
+            chunks(u, 0)
             if u == 0:
-                chunks(u, [(1, 0), (1, 1)])
-                spread_mx(0, 2)
-                spread_mx(0, 3)
-                copy_mx(0, 2)
+                chunks(u, 1)
+                spread_mx(0, 1)
+                copy_mx(0, 1)
                 prepare_g(2)
-                copy_mx(0, 3)
                 prepare_g(3)
                 prepare_v(1)
                 exp_piece(0, d_tiles[u], e_tiles[u])
-                copy_mx(0, 0)
                 pool_a(1)
                 pool_b(1)
             else:
                 exp_piece(0, d_tiles[u], e_tiles[u])
                 if u == 7:
                     eb_codes(6)
-                chunks(u, [(1, 0), (1, 1)])
+                chunks(u, 1)
                 if u == 1:
                     prepare_v(2)
                     prepare_v(3)
@@ -353,10 +367,8 @@ def tile_mex_t_kernel(tc, x, offsets, out):
                 sp1 = select_negated(1)
                 copy_negated(1, sp1)
             if u == 2 or u == 3:
-                for v in (2 * u - 4, 2 * u - 3):
-                    spread_mx(1, v)
-                for v in (2 * u - 4, 2 * u - 3):
-                    copy_mx(1, v)
+                spread_mx(1, u - 2)
+                copy_mx(1, u - 2)
             if 2 <= u < 6:
                 prepare_g(u + 2)
             if 3 <= u < 7:
@@ -372,14 +384,11 @@ def tile_mex_t_kernel(tc, x, offsets, out):
         for i in range(4):
             for mt in range(8):
                 ot = opool.tile([P, 1024], F32, name="ot")
-                last = i == 3 and mt == 7
+                last = (i == 3 and mt == 7) or (i == 0 and mt == 0)
                 for hh in range(2):
                     k = acc_no[0] % 8
                     acc_no[0] += 1
-                    if k < 4:
-                        acc = bank(k, [P, 512], F32)
-                    else:
-                        acc = ps.tile([P, 512], F32, tag="mxp%d" % (k - 4), name="ac%d" % k)
+                    acc = bank(k, [P, 512], F32)
                     for g in range(2):
                         nc.tensor.matmul_mx(
                             out=acc[:],

@@ -145,48 +145,46 @@ def tile_mex_t_kernel(tc, x, offsets, out):
 
         chunk_no = [0]
 
-        def chunk_pair(g, i, hh, e_tile):
-            dps = []
+        def unit_on_pe(i, hh):
+            dps = {}
             for b in range(2):
-                dps.append(bank(chunk_no[0] % CHUNK_BANKS, [P, 512], F32))
-                chunk_no[0] += 1
-            rows = xs[:, g, i, :].rearrange("p (h w) -> p h w", w=35)
-
-            def copy_x(b):
-                nc.tensor.matmul(
-                    out=dps[b][:].rearrange("p (r w) -> p r w", w=32),
-                    lhsT=ident[:],
-                    rhs=rows[:, 16 * hh : 16 * hh + 16, b : b + 32],
-                    start=True,
-                    stop=False,
-                )
-
-            def add_quarter(jj):
-                k = 4 * jj + i
-                nc.tensor.matmul(
-                    out=dps[1][:, jj * P : (jj + 1) * P],
-                    lhsT=negm[:, hh, 1, k : k + 1].to_broadcast([P, P]),
-                    rhs=ident32[:],
-                    is_transpose=True,
-                    start=False,
-                    stop=(jj == 3),
-                )
-
-            copy_x(1)
-            add_quarter(0)
-            copy_x(0)
-            add_quarter(1)
-            nc.tensor.matmul(
-                out=dps[0][:],
-                lhsT=mt_col[:, hh, 16 + i : 17 + i].to_broadcast([P, P]),
-                rhs=negr[:].rearrange("p q d -> p (q d)"),
-                start=False,
-                stop=True,
-            )
-            add_quarter(2)
-            add_quarter(3)
+                for g in range(2):
+                    dps[(g, b)] = bank(chunk_no[0] % CHUNK_BANKS, [P, 512], F32)
+                    chunk_no[0] += 1
             for b in range(2):
-                nc.scalar.activation(out=e_tile[:, g, b * 512 : (b + 1) * 512], in_=dps[b][:], func=ACT.Exp)
+                for g in range(2):
+                    rows = xs[:, g, i, :].rearrange("p (h w) -> p h w", w=35)
+                    nc.tensor.matmul(
+                        out=dps[(g, b)][:].rearrange("p (r w) -> p r w", w=32),
+                        lhsT=ident[:],
+                        rhs=rows[:, 16 * hh : 16 * hh + 16, b : b + 32],
+                        start=True,
+                        stop=False,
+                    )
+                    if b == 0:
+                        nc.tensor.matmul(
+                            out=dps[(g, b)][:],
+                            lhsT=mt_col[:, hh, 16 + i : 17 + i].to_broadcast([P, P]),
+                            rhs=negr[:].rearrange("p q d -> p (q d)"),
+                            start=False,
+                            stop=True,
+                        )
+            for g in range(2):
+                for jj in range(4):
+                    k = 4 * jj + i
+                    nc.tensor.matmul(
+                        out=dps[(g, 1)][:, jj * P : (jj + 1) * P],
+                        lhsT=negm[:, hh, 1, k : k + 1].to_broadcast([P, P]),
+                        rhs=ident32[:],
+                        is_transpose=True,
+                        start=False,
+                        stop=(jj == 3),
+                    )
+            return dps
+
+        def exp_chunks(dps, b, e_tile):
+            for g in range(2):
+                nc.scalar.activation(out=e_tile[:, g, b * 512 : (b + 1) * 512], in_=dps[(g, b)][:], func=ACT.Exp)
 
         def subtract(eng, m_ap, i, hh, b, d_tile):
             eng.tensor_tensor(
@@ -317,10 +315,6 @@ def tile_mex_t_kernel(tc, x, offsets, out):
             hh, i = units[u]
             subtract(nc.vector, mx_psum(u), i, hh, 2, d_tiles[u])
 
-        def chunks(u, g):
-            hh, i = units[u]
-            chunk_pair(g, i, hh, e_tiles[u])
-
         def eb_codes(mt):
             et = transpose_eb(mt)
             if mt % 2 == 0:
@@ -338,9 +332,10 @@ def tile_mex_t_kernel(tc, x, offsets, out):
         for u in range(8):
             hh, i = units[u]
             e_tiles[u] = epool.tile([P, 2, 2048], BF16, name="et_ex", align_bytes=64)
-            chunks(u, 0)
+            dps = unit_on_pe(i, hh)
+            exp_chunks(dps, 0, e_tiles[u])
             if u == 0:
-                chunks(u, 1)
+                exp_chunks(dps, 1, e_tiles[u])
                 spread_mx(0, 1)
                 copy_mx(0, 1)
                 prepare_g(2)
@@ -353,7 +348,7 @@ def tile_mex_t_kernel(tc, x, offsets, out):
                 exp_piece(0, d_tiles[u], e_tiles[u])
                 if u == 7:
                     eb_codes(6)
-                chunks(u, 1)
+                exp_chunks(dps, 1, e_tiles[u])
                 if u == 1:
                     prepare_v(2)
                     prepare_v(3)

@@ -41,6 +41,7 @@ def tile_mex_t_kernel(tc, x, offsets, out):
         tr1 = keep.tile([P, 4, 512], BF16)
         tr2 = keep.tile([P, 4, 256], BF16)
         tr3 = keep.tile([P, 4, 128], BF16)
+        warm = keep.tile([P, 1], F32)
         nmb = keep.tile([P, 8], F32)
         mbc = keep.tile([P, 8], F32)
         ebp = keep.tile([P, 8, 1024], BF16)
@@ -214,9 +215,9 @@ def tile_mex_t_kernel(tc, x, offsets, out):
                 op=ALU.subtract,
             )
 
-        def exp_piece(g, d_tile, e_tile):
+        def exp_piece(d_tile, e_tile):
             nc.scalar.activation(
-                out=e_tile[:, g, 1024:2048], in_=d_tile[:, g].rearrange("p b n -> p (b n)"), func=ACT.Exp
+                out=e_tile[:, :, 1024:2048], in_=d_tile[:].rearrange("p g b n -> p g (b n)"), func=ACT.Exp
             )
 
         def quantise_ex(hh, i, e_tile):
@@ -248,8 +249,9 @@ def tile_mex_t_kernel(tc, x, offsets, out):
                     in_=ebg[:, g].rearrange("p m v -> p (m v)").bitcast(BF16),
                 )
 
-        make_identity(nc, ident[:])
         nc.vector.memset(mt_col[:], 0.0)
+        nc.scalar.activation(out=warm[:], in_=mt_col[:, 0, 0:1], func=ACT.Exp)
+        make_identity(nc, ident[:])
         nc.vector.tensor_copy(out=ident32[:], in_=ident[:])
         nc.vector.tensor_scalar_mul(out=negr[:], in0=ident[:].unsqueeze(2).to_broadcast([P, P, 4]), scalar1=-1.0)
         for b in range(4):
@@ -341,18 +343,16 @@ def tile_mex_t_kernel(tc, x, offsets, out):
                 prepare_g(2)
                 prepare_g(3)
                 prepare_v(1)
-                exp_piece(0, d_tiles[u], e_tiles[u])
                 pool_a(1)
                 pool_b(1)
             else:
-                exp_piece(0, d_tiles[u], e_tiles[u])
                 if u == 7:
                     eb_codes(6)
                 exp_chunks(dps, 1, e_tiles[u])
                 if u == 1:
                     prepare_v(2)
                     prepare_v(3)
-            exp_piece(1, d_tiles[u], e_tiles[u])
+            exp_piece(d_tiles[u], e_tiles[u])
             if u == 0:
                 eb_codes(0)
             if u == 1:

@@ -47,16 +47,18 @@ def tile_mex_t_kernel(tc, x, offsets, out):
         ebp = keep.tile([P, 8, 1024], BF16)
         ebc = keep.tile([P, 2, 1024], U32, align_bytes=64)
         ebs = keep.tile([P, 2, 1024], U8, align_bytes=64)
-        xq = keep.tile([P, 2, 1225], BF16)
-        t0 = keep.tile([P, 665], BF16)
-        t1 = keep.tile([P, 665], BF16)
-        t2 = keep.tile([P, 665], BF16)
-        t3 = keep.tile([P, 665], BF16)
+        xq = keep.tile([P, 2, 1232], BF16)
+        t0 = keep.tile([P, 2, 666], BF16)
+        t1 = keep.tile([P, 2, 666], BF16)
+        t2 = keep.tile([P, 2, 666], BF16)
+        t3 = keep.tile([P, 2, 666], BF16)
         p4 = keep.tile([P, 2, 512], BF16)
         mt_col = keep.tile([P, 2, 32], BF16)
         negm = keep.tile([P, 2, 4, 32], F32)
         mxs = keep.tile([P, 4, 1024], BF16)
-        xs = keep.tile([P, 2, 4, 1120], BF16)
+        xs01 = keep.tile([P, 2, 2, 1120], BF16)
+        xs23 = keep.tile([P, 2, 2, 1120], BF16)
+        xs = [xs01, xs23]
         exc = keep.tile([P, 8, 2, 512], U32, align_bytes=64)
         exs = keep.tile([P, 8, 2, 512], U8, align_bytes=64)
         CHUNK_BANKS = 5
@@ -71,18 +73,23 @@ def tile_mex_t_kernel(tc, x, offsets, out):
             for g in range(2):
                 for dh in range(4):
                     nc.sync.dma_start(
-                        out=xs[dh:P:4, g, 2 * pr : 2 * pr + 2, :],
+                        out=xs[pr][dh:P:4, :, g, :],
                         in_=x[2 * pr : 2 * pr + 2, 32 * g : 32 * g + 32, dh : dh + 32, :].rearrange(
                             "i c h w -> c i (h w)"
                         ),
                     )
 
-        def max_of_b(m0, n):
+        def max_step(level, m0, n, s0):
             s = slice(m0, m0 + n)
-            nc.vector.tensor_max(out=tr1[:, 0:n, :], in0=b_sb[:, s, 0:512], in1=b_sb[:, s, 512:1024])
-            nc.vector.tensor_max(out=tr2[:, 0:n, :], in0=tr1[:, 0:n, 0:256], in1=tr1[:, 0:n, 256:512])
-            nc.vector.tensor_max(out=tr3[:, 0:n, :], in0=tr2[:, 0:n, 0:128], in1=tr2[:, 0:n, 128:256])
-            nc.vector.tensor_reduce(out=nmb[:, s], in_=tr3[:, 0:n, :], axis=AX.X, op=ALU.max, negate=True)
+            q = slice(s0, s0 + n)
+            if level == 1:
+                nc.vector.tensor_max(out=tr1[:, q, :], in0=b_sb[:, s, 0:512], in1=b_sb[:, s, 512:1024])
+            elif level == 2:
+                nc.vector.tensor_max(out=tr2[:, q, :], in0=tr1[:, q, 0:256], in1=tr1[:, q, 256:512])
+            elif level == 3:
+                nc.vector.tensor_max(out=tr3[:, q, :], in0=tr2[:, q, 0:128], in1=tr2[:, q, 128:256])
+            else:
+                nc.vector.tensor_reduce(out=nmb[:, s], in_=tr3[:, q, :], axis=AX.X, op=ALU.max, negate=True)
 
         def exp_of_b(mt):
             nc.scalar.activation(
@@ -93,19 +100,22 @@ def tile_mex_t_kernel(tc, x, offsets, out):
                 scale=1.0,
             )
 
-        def pool_a(hh):
+        def pool_step(step, hh):
             f0 = 560 * hh
-            nc.vector.tensor_max(out=t0[:], in0=xq[:, 0, f0 : f0 + 665], in1=xq[:, 1, f0 : f0 + 665])
-            nc.vector.tensor_max(out=t1[:, 0:664], in0=t0[:, 0:664], in1=t0[:, 1:665])
-            nc.vector.tensor_max(out=t2[:, 0:662], in0=t1[:, 0:662], in1=t1[:, 2:664])
-
-        def pool_b(hh):
-            nc.vector.tensor_max(out=t3[:, 0:627], in0=t2[:, 0:627], in1=t2[:, 35:662])
-            nc.vector.tensor_max(
-                out=p4[:, hh, :].rearrange("p (h w) -> p h w", w=32),
-                in0=t3[:, 0:560].rearrange("p (h w) -> p h w", w=35)[:, :, 0:32],
-                in1=t3[:, 70:630].rearrange("p (h w) -> p h w", w=35)[:, :, 0:32],
-            )
+            if step == 1:
+                nc.vector.tensor_max(out=t0[:, hh, 0:665], in0=xq[:, 0, f0 : f0 + 665], in1=xq[:, 1, f0 : f0 + 665])
+            elif step == 2:
+                nc.vector.tensor_max(out=t1[:, hh, 0:664], in0=t0[:, hh, 0:664], in1=t0[:, hh, 1:665])
+            elif step == 3:
+                nc.vector.tensor_max(out=t2[:, hh, 0:662], in0=t1[:, hh, 0:662], in1=t1[:, hh, 2:664])
+            elif step == 4:
+                nc.vector.tensor_max(out=t3[:, hh, 0:627], in0=t2[:, hh, 0:627], in1=t2[:, hh, 35:662])
+            else:
+                nc.vector.tensor_max(
+                    out=p4[:, hh, :].rearrange("p (h w) -> p h w", w=32),
+                    in0=t3[:, hh, 0:560].rearrange("p (h w) -> p h w", w=35)[:, :, 0:32],
+                    in1=t3[:, hh, 70:630].rearrange("p (h w) -> p h w", w=35)[:, :, 0:32],
+                )
 
         def transpose_pooled(hh):
             pt = bank(SIDE_BANK, [P, 5, P], BF16)
@@ -132,9 +142,10 @@ def tile_mex_t_kernel(tc, x, offsets, out):
         def copy_negated(hh, selp):
             nc.vector.tensor_copy(out=negm[:, hh], in_=selp[:])
 
-        def spread_mx(hh, pr):
-            mxp[pr] = bank(MX_BANK + pr, [P, 2, 512], BF16)
-            for il in range(2):
+        def spread_mx(hh, pr, ils=(0, 1)):
+            if 0 in ils:
+                mxp[pr] = bank(MX_BANK + pr, [P, 2, 512], BF16)
+            for il in ils:
                 for jj in range(4):
                     k = 4 * jj + 2 * pr + il
                     nc.tensor.transpose(
@@ -146,30 +157,34 @@ def tile_mex_t_kernel(tc, x, offsets, out):
 
         chunk_no = [0]
 
-        def unit_on_pe(i, hh):
+        def unit_banks():
             dps = {}
             for b in range(2):
                 for g in range(2):
                     dps[(g, b)] = bank(chunk_no[0] % CHUNK_BANKS, [P, 512], F32)
                     chunk_no[0] += 1
-            for b in range(2):
-                for g in range(2):
-                    rows = xs[:, g, i, :].rearrange("p (h w) -> p h w", w=35)
-                    nc.tensor.matmul(
-                        out=dps[(g, b)][:].rearrange("p (r w) -> p r w", w=32),
-                        lhsT=ident[:],
-                        rhs=rows[:, 16 * hh : 16 * hh + 16, b : b + 32],
-                        start=True,
-                        stop=False,
-                    )
-                    if b == 0:
-                        nc.tensor.matmul(
-                            out=dps[(g, b)][:],
-                            lhsT=mt_col[:, hh, 16 + i : 17 + i].to_broadcast([P, P]),
-                            rhs=negr[:].rearrange("p q d -> p (q d)"),
-                            start=False,
-                            stop=True,
-                        )
+            return dps
+
+        def copy_x(dps, g, b, i, hh):
+            rows = xs[i // 2][:, i % 2, g, :].rearrange("p (h w) -> p h w", w=35)
+            nc.tensor.matmul(
+                out=dps[(g, b)][:].rearrange("p (r w) -> p r w", w=32),
+                lhsT=ident[:],
+                rhs=rows[:, 16 * hh : 16 * hh + 16, b : b + 32],
+                start=True,
+                stop=False,
+            )
+
+        def add_class0(dps, g, i, hh):
+            nc.tensor.matmul(
+                out=dps[(g, 0)][:],
+                lhsT=mt_col[:, hh, 16 + i : 17 + i].to_broadcast([P, P]),
+                rhs=negr[:].rearrange("p q d -> p (q d)"),
+                start=False,
+                stop=True,
+            )
+
+        def unit_add_class1(dps, i, hh):
             for g in range(2):
                 for jj in range(4):
                     k = 4 * jj + i
@@ -181,16 +196,25 @@ def tile_mex_t_kernel(tc, x, offsets, out):
                         start=False,
                         stop=(jj == 3),
                     )
+
+        def unit_on_pe(i, hh):
+            dps = unit_banks()
+            for g in range(2):
+                copy_x(dps, g, 0, i, hh)
+                add_class0(dps, g, i, hh)
+            for g in range(2):
+                copy_x(dps, g, 1, i, hh)
+            unit_add_class1(dps, i, hh)
             return dps
 
         def exp_chunks(dps, b, e_tile):
             for g in range(2):
                 nc.scalar.activation(out=e_tile[:, g, b * 512 : (b + 1) * 512], in_=dps[(g, b)][:], func=ACT.Exp)
 
-        def subtract(eng, m_ap, i, hh, b, d_tile):
+        def subtract(eng, m_ap, i, hh, b, d_view):
             eng.tensor_tensor(
-                out=d_tile[:, :, b - 2, :].rearrange("p g (hl a d) -> p g hl a d", a=8, d=4),
-                in0=xs[:, :, i, :]
+                out=d_view.rearrange("p g (hl a d) -> p g hl a d", a=8, d=4),
+                in0=xs[i // 2][:, i % 2, :, :]
                 .rearrange("p g (h w) -> p g h w", w=35)[:, :, 16 * hh : 16 * hh + 16, b : b + 32]
                 .rearrange("p g hl (a d) -> p g hl a d", d=4),
                 in1=m_ap
@@ -204,8 +228,8 @@ def tile_mex_t_kernel(tc, x, offsets, out):
         def subtract_part(eng, m_ap, i, hh, b, d_tile, g, q):
             h0 = 16 * hh + 8 * q
             eng.tensor_tensor(
-                out=d_tile[:, g, b - 2, 256 * q : 256 * q + 256].rearrange("p (hl a d) -> p hl a d", a=8, d=4),
-                in0=xs[:, g, i, :]
+                out=d_tile[:, b - 2, g, 256 * q : 256 * q + 256].rearrange("p (hl a d) -> p hl a d", a=8, d=4),
+                in0=xs[i // 2][:, i % 2, g, :]
                 .rearrange("p (h w) -> p h w", w=35)[:, h0 : h0 + 8, b : b + 32]
                 .rearrange("p hl (a d) -> p hl a d", d=4),
                 in1=m_ap[:, 256 * q : 256 * q + 256]
@@ -217,8 +241,13 @@ def tile_mex_t_kernel(tc, x, offsets, out):
 
         def exp_piece(d_tile, e_tile):
             nc.scalar.activation(
-                out=e_tile[:, :, 1024:2048], in_=d_tile[:].rearrange("p g b n -> p g (b n)"), func=ACT.Exp
+                out=e_tile[:, :, 1024:2048].rearrange("p g (b n) -> p g b n", b=2),
+                in_=d_tile[:].rearrange("p b g n -> p g b n"),
+                func=ACT.Exp,
             )
+
+        def exp_class(b, d_tile, e_tile):
+            nc.scalar.activation(out=e_tile[:, :, b * 512 : (b + 1) * 512], in_=d_tile[:, b - 2], func=ACT.Exp)
 
         def quantise_ex(hh, i, e_tile):
             nc.vector.quantize_mx(
@@ -267,31 +296,51 @@ def tile_mex_t_kernel(tc, x, offsets, out):
         nc.sync.dma_start(out=b_sb[:, 0:1, :], in_=bv[:, 0:1, :])
         nc.sync.dma_start(out=b_sb[:, 1:2, :], in_=bv[:, 1:2, :])
         nc.sync.dma_start(out=b_sb[:, 2:4, :], in_=bv[:, 2:4, :])
-        nc.sync.dma_start(out=xq[:], in_=xq_v)
+        nc.sync.dma_start(out=xq[:, :, 0:672], in_=xq_v[:, :, 0:672])
         nc.sync.dma_start(out=b_sb[:, 4:6, :], in_=bv[:, 4:6, :])
         nc.sync.dma_start(out=b_sb[:, 6:8, :], in_=bv[:, 6:8, :])
+        nc.sync.dma_start(out=xq[:, :, 672:1225], in_=xq_v[:, :, 672:1225])
         load_x_rows(0)
         load_x_rows(1)
 
-        max_of_b(0, 1)
+        tree_a, tree_b, tree_c, tree_e, tree_f = (0, 1, 0), (1, 1, 1), (2, 2, 2), (4, 2, 0), (6, 2, 2)
+        for level in range(1, 5):
+            max_step(level, *tree_a)
+            max_step(level, *tree_b)
         exp_of_b(0)
-        max_of_b(1, 1)
         exp_of_b(1)
-        max_of_b(2, 2)
+        for level in range(1, 4):
+            max_step(level, *tree_c)
+            pool_step(level, 0)
+        max_step(4, *tree_c)
         exp_of_b(2)
         exp_of_b(3)
-        pool_a(0)
-        max_of_b(4, 2)
+        max_step(1, *tree_e)
+        pool_step(4, 0)
+        max_step(2, *tree_e)
+        pool_step(5, 0)
+        pt0 = transpose_pooled(0)
+        dps0 = unit_banks()
+        for g in range(2):
+            copy_x(dps0, g, 0, 0, 0)
+        max_step(3, *tree_e)
+        max_step(1, *tree_f)
+        max_step(4, *tree_e)
         exp_of_b(4)
         exp_of_b(5)
-        pool_b(0)
-        pt0 = transpose_pooled(0)
-        max_of_b(6, 2)
+        max_step(2, *tree_f)
+        max_over_channels(0, pt0)
+        spread_mx(0, 0, (0,))
+        for g in range(2):
+            add_class0(dps0, g, 0, 0)
+        sp0 = select_negated(0)
+        for g in range(2):
+            copy_x(dps0, g, 1, 0, 0)
+        max_step(3, *tree_f)
+        pool_step(1, 1)
+        max_step(4, *tree_f)
         exp_of_b(6)
         exp_of_b(7)
-        max_over_channels(0, pt0)
-        sp0 = select_negated(0)
-        copy_negated(0, sp0)
 
         units = [(hh, i) for hh in range(2) for i in range(4)]
         d_tiles = {}
@@ -315,7 +364,7 @@ def tile_mex_t_kernel(tc, x, offsets, out):
 
         def prepare_v(u):
             hh, i = units[u]
-            subtract(nc.vector, mx_psum(u), i, hh, 2, d_tiles[u])
+            subtract(nc.vector, mx_psum(u), i, hh, 2, d_tiles[u][:, 0])
 
         def eb_codes(mt):
             et = transpose_eb(mt)
@@ -325,34 +374,58 @@ def tile_mex_t_kernel(tc, x, offsets, out):
             if mt % 2 == 1:
                 quantise_eb(mt // 2, ebg_now[0])
 
-        spread_mx(0, 0)
-        copy_mx(0, 0)
-        prepare_g(1)
+        ACC_ORDER = [6, 7, 2, 5, 3, 4, 0, 1]
+        sums = {}
+
+        def mx_group(i, mt, hh):
+            acc = bank(ACC_ORDER[len(sums) % 8], [P, 512], F32)
+            sums[(i, mt, hh)] = acc
+            for g in range(2):
+                nc.tensor.matmul_mx(
+                    out=acc[:],
+                    lhsT=ebc[:, g, mt * P : (mt + 1) * P].bitcast(FP8X4),
+                    lhsT_scale=ebs[:, g, mt * P : (mt + 1) * P],
+                    rhs=exc[:, 2 * i + hh, g, :].bitcast(FP8X4),
+                    rhs_scale=exs[:, 2 * i + hh, g, :],
+                    start=(g == 0),
+                    stop=(g == 1),
+                )
+
         d_tiles[0] = dpool.tile([P, 2, 2, 512], F32, name="dt")
-        subtract(nc.vector, mx_psum(0), 0, 0, 2, d_tiles[0])
-        subtract(nc.vector, mx_psum(0), 0, 0, 3, d_tiles[0])
+        subtract(nc.vector, mx_psum(0), 0, 0, 2, d_tiles[0][:, 0])
+        pool_step(2, 1)
+        copy_negated(0, sp0)
+        pool_step(3, 1)
+        subtract(nc.vector, mx_psum(0), 0, 0, 3, d_tiles[0][:, 1])
+        pool_step(4, 1)
+        unit_add_class1(dps0, 0, 0)
         for u in range(8):
             hh, i = units[u]
             e_tiles[u] = epool.tile([P, 2, 2048], BF16, name="et_ex", align_bytes=64)
-            dps = unit_on_pe(i, hh)
+            dps = dps0 if u == 0 else unit_on_pe(i, hh)
             exp_chunks(dps, 0, e_tiles[u])
             if u == 0:
+                exp_class(2, d_tiles[u], e_tiles[u])
                 exp_chunks(dps, 1, e_tiles[u])
-                spread_mx(0, 1)
-                copy_mx(0, 1)
-                prepare_g(2)
-                prepare_g(3)
+                exp_class(3, d_tiles[u], e_tiles[u])
+                spread_mx(0, 0, (1,))
+                copy_mx(0, 0)
+                prepare_g(1)
+                pool_step(5, 1)
                 prepare_v(1)
-                pool_a(1)
-                pool_b(1)
             else:
+                if u == 1:
+                    spread_mx(0, 1)
+                    copy_mx(0, 1)
+                    prepare_g(2)
+                    prepare_g(3)
                 if u == 7:
                     eb_codes(6)
                 exp_chunks(dps, 1, e_tiles[u])
                 if u == 1:
                     prepare_v(2)
                     prepare_v(3)
-            exp_piece(d_tiles[u], e_tiles[u])
+                exp_piece(d_tiles[u], e_tiles[u])
             if u == 0:
                 eb_codes(0)
             if u == 1:
@@ -368,6 +441,9 @@ def tile_mex_t_kernel(tc, x, offsets, out):
                 prepare_g(u + 2)
             if 3 <= u < 7:
                 prepare_v(u + 1)
+            if u == 7:
+                for early in ((0, 0, 0), (0, 0, 1), (0, 1, 0)):
+                    mx_group(*early)
             if u >= 2:
                 eb_codes(u - 1 if u < 7 else 7)
             quantise_ex(hh, i, e_tiles[u])
@@ -375,25 +451,14 @@ def tile_mex_t_kernel(tc, x, offsets, out):
             out=mbc[:], in0=nmb[:], scalar1=-1.0, scalar2=-math.log(1024.0), op0=ALU.mult, op1=ALU.add
         )
 
-        acc_no = [0]
         for i in range(4):
             for mt in range(8):
                 ot = opool.tile([P, 1024], F32, name="ot")
                 last = (i == 3 and mt == 7) or (i == 0 and mt == 0)
                 for hh in range(2):
-                    k = acc_no[0] % 8
-                    acc_no[0] += 1
-                    acc = bank(k, [P, 512], F32)
-                    for g in range(2):
-                        nc.tensor.matmul_mx(
-                            out=acc[:],
-                            lhsT=ebc[:, g, mt * P : (mt + 1) * P].bitcast(FP8X4),
-                            lhsT_scale=ebs[:, g, mt * P : (mt + 1) * P],
-                            rhs=exc[:, 2 * i + hh, g, :].bitcast(FP8X4),
-                            rhs_scale=exs[:, 2 * i + hh, g, :],
-                            start=(g == 0),
-                            stop=(g == 1),
-                        )
+                    if (i, mt, hh) not in sums:
+                        mx_group(i, mt, hh)
+                    acc = sums[(i, mt, hh)]
                     nc.scalar.activation(
                         out=ot[:, hh * 512 : (hh + 1) * 512].rearrange("p (hl a bb) -> p hl a bb", a=8, bb=4),
                         in_=acc[:].rearrange("p (bb hl a) -> p hl a bb", bb=4, a=8),

@@ -61,23 +61,26 @@ def tile_mex_t_kernel(tc, x, offsets, out):
         xs = [xs01, xs23]
         exc = keep.tile([P, 8, 2, 512], U32, align_bytes=64)
         exs = keep.tile([P, 8, 2, 512], U8, align_bytes=64)
-        CHUNK_BANKS = 5
-        SIDE_BANK = 5
+        CHUNK_BANKS = 4
+        SIDE_BANKS = (4, 5)
+        side_no = [0]
         MX_BANK = 6
         mxp = [None, None]
 
         def bank(k, shape, dtype):
             return ps.tile(shape, dtype, tag="bank%d" % k, name="bk%d" % k)
 
+        def side_bank(shape, dtype):
+            side_no[0] += 1
+            return bank(SIDE_BANKS[side_no[0] % 2], shape, dtype)
+
         def load_x_rows(pr):
-            for g in range(2):
-                for dh in range(4):
-                    nc.sync.dma_start(
-                        out=xs[pr][dh:P:4, :, g, :],
-                        in_=x[2 * pr : 2 * pr + 2, 32 * g : 32 * g + 32, dh : dh + 32, :].rearrange(
-                            "i c h w -> c i (h w)"
-                        ),
-                    )
+            rows = x[2 * pr : 2 * pr + 2].rearrange("i (g c) h w -> c (i g) (h w)", g=2)
+            for dh in range(4):
+                nc.sync.dma_start(
+                    out=xs[pr][dh:P:4].rearrange("p i g n -> p (i g) n"),
+                    in_=rows[:, :, 35 * dh : 35 * dh + 1120],
+                )
 
         def max_step(level, m0, n, s0):
             s = slice(m0, m0 + n)
@@ -86,10 +89,8 @@ def tile_mex_t_kernel(tc, x, offsets, out):
                 nc.vector.tensor_max(out=tr1[:, q, :], in0=b_sb[:, s, 0:512], in1=b_sb[:, s, 512:1024])
             elif level == 2:
                 nc.vector.tensor_max(out=tr2[:, q, :], in0=tr1[:, q, 0:256], in1=tr1[:, q, 256:512])
-            elif level == 3:
-                nc.vector.tensor_max(out=tr3[:, q, :], in0=tr2[:, q, 0:128], in1=tr2[:, q, 128:256])
             else:
-                nc.vector.tensor_reduce(out=nmb[:, s], in_=tr3[:, q, :], axis=AX.X, op=ALU.max, negate=True)
+                nc.vector.tensor_reduce(out=nmb[:, s], in_=tr2[:, q, :], axis=AX.X, op=ALU.max, negate=True)
 
         def exp_of_b(mt):
             nc.scalar.activation(
@@ -118,7 +119,7 @@ def tile_mex_t_kernel(tc, x, offsets, out):
                 )
 
         def transpose_pooled(hh):
-            pt = bank(SIDE_BANK, [P, 5, P], BF16)
+            pt = side_bank([P, 5, P], BF16)
             for jj in range(4):
                 nc.tensor.transpose(pt[:, jj, :], p4[:, hh, jj * P : (jj + 1) * P], ident[:])
             nc.tensor.transpose(pt[:, 4, :], p4[:, hh, :].rearrange("p (q bb) -> p q bb", bb=4)[:, :, 0], ident[:])
@@ -134,7 +135,7 @@ def tile_mex_t_kernel(tc, x, offsets, out):
                 )
 
         def select_negated(hh):
-            selp = bank(SIDE_BANK, [P, 4, 32], F32)
+            selp = side_bank([P, 4, 32], F32)
             for b in range(4):
                 nc.tensor.matmul(out=selp[:, b, :], lhsT=nsel[:, b, :], rhs=mt_col[:, hh, :], start=True, stop=True)
             return selp
@@ -197,11 +198,13 @@ def tile_mex_t_kernel(tc, x, offsets, out):
                         stop=(jj == 3),
                     )
 
-        def unit_on_pe(i, hh):
+        def unit_on_pe(i, hh, between=None):
             dps = unit_banks()
             for g in range(2):
                 copy_x(dps, g, 0, i, hh)
                 add_class0(dps, g, i, hh)
+            if between:
+                between()
             for g in range(2):
                 copy_x(dps, g, 1, i, hh)
             unit_add_class1(dps, i, hh)
@@ -257,7 +260,7 @@ def tile_mex_t_kernel(tc, x, offsets, out):
             )
 
         def transpose_eb(mt):
-            et = bank(SIDE_BANK, [P, 4, P], F32)
+            et = side_bank([P, 4, P], F32)
             words = ebp[:, mt, :].bitcast(F32)
             for g in range(2):
                 for v in range(2):
@@ -298,37 +301,42 @@ def tile_mex_t_kernel(tc, x, offsets, out):
         nc.sync.dma_start(out=b_sb[:, 2:4, :], in_=bv[:, 2:4, :])
         nc.sync.dma_start(out=xq[:, :, 0:672], in_=xq_v[:, :, 0:672])
         nc.sync.dma_start(out=b_sb[:, 4:6, :], in_=bv[:, 4:6, :])
-        nc.sync.dma_start(out=b_sb[:, 6:8, :], in_=bv[:, 6:8, :])
-        nc.sync.dma_start(out=xq[:, :, 672:1225], in_=xq_v[:, :, 672:1225])
         load_x_rows(0)
+        nc.sync.dma_start(out=xq[:, :, 672:1225], in_=xq_v[:, :, 672:1225])
+        nc.sync.dma_start(out=b_sb[:, 6:8, :], in_=bv[:, 6:8, :])
         load_x_rows(1)
 
-        tree_a, tree_b, tree_c, tree_e, tree_f = (0, 1, 0), (1, 1, 1), (2, 2, 2), (4, 2, 0), (6, 2, 2)
-        for level in range(1, 5):
-            max_step(level, *tree_a)
-            max_step(level, *tree_b)
+        max_step(1, 0, 1, 0)
+        max_step(2, 0, 1, 0)
+        max_step(1, 1, 1, 1)
+        max_step(3, 0, 1, 0)
         exp_of_b(0)
+        max_step(2, 1, 1, 1)
+        max_step(1, 2, 1, 2)
+        max_step(3, 1, 1, 1)
         exp_of_b(1)
-        for level in range(1, 4):
-            max_step(level, *tree_c)
-            pool_step(level, 0)
-        max_step(4, *tree_c)
+        pool_step(1, 0)
+        max_step(2, 2, 1, 2)
+        max_step(1, 3, 1, 3)
+        pool_step(2, 0)
+        max_step(3, 2, 1, 2)
         exp_of_b(2)
-        exp_of_b(3)
-        max_step(1, *tree_e)
+        pool_step(3, 0)
+        max_step(2, 3, 1, 3)
+        max_step(1, 4, 1, 0)
         pool_step(4, 0)
-        max_step(2, *tree_e)
+        max_step(3, 3, 1, 3)
+        exp_of_b(3)
         pool_step(5, 0)
         pt0 = transpose_pooled(0)
         dps0 = unit_banks()
         for g in range(2):
             copy_x(dps0, g, 0, 0, 0)
-        max_step(3, *tree_e)
-        max_step(1, *tree_f)
-        max_step(4, *tree_e)
+        max_step(2, 4, 1, 0)
+        max_step(1, 5, 1, 1)
+        max_step(3, 4, 1, 0)
         exp_of_b(4)
-        exp_of_b(5)
-        max_step(2, *tree_f)
+        max_step(2, 5, 1, 1)
         max_over_channels(0, pt0)
         spread_mx(0, 0, (0,))
         for g in range(2):
@@ -336,11 +344,9 @@ def tile_mex_t_kernel(tc, x, offsets, out):
         sp0 = select_negated(0)
         for g in range(2):
             copy_x(dps0, g, 1, 0, 0)
-        max_step(3, *tree_f)
+        max_step(3, 5, 1, 1)
+        exp_of_b(5)
         pool_step(1, 1)
-        max_step(4, *tree_f)
-        exp_of_b(6)
-        exp_of_b(7)
 
         units = [(hh, i) for hh in range(2) for i in range(4)]
         d_tiles = {}
@@ -358,13 +364,16 @@ def tile_mex_t_kernel(tc, x, offsets, out):
         def prepare_g(u):
             hh, i = units[u]
             d_tiles[u] = dpool.tile([P, 2, 2, 512], F32, name="dt")
-            for g in range(2):
-                for q in range(2):
-                    subtract_part(nc.gpsimd, mx_sbuf(u), i, hh, 3, d_tiles[u], g, q)
+            if u not in (1, 3, 5, 7):
+                for g in range(2):
+                    for q in range(2):
+                        subtract_part(nc.gpsimd, mx_sbuf(u), i, hh, 3, d_tiles[u], g, q)
 
         def prepare_v(u):
             hh, i = units[u]
             subtract(nc.vector, mx_psum(u), i, hh, 2, d_tiles[u][:, 0])
+            if u in (1, 3, 5, 7):
+                subtract(nc.vector, mx_psum(u), i, hh, 3, d_tiles[u][:, 1])
 
         def eb_codes(mt):
             et = transpose_eb(mt)
@@ -374,7 +383,7 @@ def tile_mex_t_kernel(tc, x, offsets, out):
             if mt % 2 == 1:
                 quantise_eb(mt // 2, ebg_now[0])
 
-        ACC_ORDER = [6, 7, 2, 5, 3, 4, 0, 1]
+        ACC_ORDER = [6, 7, 5, 4, 0, 1, 2, 3]
         sums = {}
 
         def mx_group(i, mt, hh):
@@ -395,43 +404,48 @@ def tile_mex_t_kernel(tc, x, offsets, out):
         subtract(nc.vector, mx_psum(0), 0, 0, 2, d_tiles[0][:, 0])
         pool_step(2, 1)
         copy_negated(0, sp0)
-        pool_step(3, 1)
+        max_step(1, 6, 2, 2)
         subtract(nc.vector, mx_psum(0), 0, 0, 3, d_tiles[0][:, 1])
+        max_step(2, 6, 2, 2)
+        pool_step(3, 1)
+        max_step(3, 6, 2, 2)
         pool_step(4, 1)
         unit_add_class1(dps0, 0, 0)
+        eb_of_unit = {2: (0,), 3: (1,), 4: (2, 3), 5: (4,), 6: (5, 6), 7: (7,)}
         for u in range(8):
             hh, i = units[u]
             e_tiles[u] = epool.tile([P, 2, 2048], BF16, name="et_ex", align_bytes=64)
-            dps = dps0 if u == 0 else unit_on_pe(i, hh)
+            if u == 0:
+                dps = dps0
+            elif u == 1:
+                dps = unit_on_pe(i, hh, lambda: spread_mx(0, 1))
+            else:
+                dps = unit_on_pe(i, hh)
             exp_chunks(dps, 0, e_tiles[u])
             if u == 0:
                 exp_class(2, d_tiles[u], e_tiles[u])
                 exp_chunks(dps, 1, e_tiles[u])
                 exp_class(3, d_tiles[u], e_tiles[u])
+                exp_of_b(6)
+                exp_of_b(7)
                 spread_mx(0, 0, (1,))
+                pool_step(5, 1)
                 copy_mx(0, 0)
                 prepare_g(1)
-                pool_step(5, 1)
                 prepare_v(1)
             else:
                 if u == 1:
-                    spread_mx(0, 1)
                     copy_mx(0, 1)
                     prepare_g(2)
                     prepare_g(3)
-                if u == 7:
-                    eb_codes(6)
                 exp_chunks(dps, 1, e_tiles[u])
-                if u == 1:
-                    prepare_v(2)
-                    prepare_v(3)
                 exp_piece(d_tiles[u], e_tiles[u])
-            if u == 0:
-                eb_codes(0)
             if u == 1:
+                prepare_v(2)
                 pt1 = transpose_pooled(1)
                 max_over_channels(1, pt1)
-            if u == 2:
+                prepare_v(3)
+            if u == 3:
                 sp1 = select_negated(1)
                 copy_negated(1, sp1)
             if u == 2 or u == 3:
@@ -444,8 +458,8 @@ def tile_mex_t_kernel(tc, x, offsets, out):
             if u == 7:
                 for early in ((0, 0, 0), (0, 0, 1), (0, 1, 0)):
                     mx_group(*early)
-            if u >= 2:
-                eb_codes(u - 1 if u < 7 else 7)
+            for mt in eb_of_unit.get(u, ()):
+                eb_codes(mt)
             quantise_ex(hh, i, e_tiles[u])
         nc.vector.tensor_scalar(
             out=mbc[:], in0=nmb[:], scalar1=-1.0, scalar2=-math.log(1024.0), op0=ALU.mult, op1=ALU.add

@@ -25,7 +25,7 @@ def tile_mex_t_kernel(tc, x, offsets, out):
         dpool = ctx.enter_context(tc.tile_pool(name="dpool", bufs=4))
         epool = ctx.enter_context(tc.tile_pool(name="epool", bufs=3))
         gpool = ctx.enter_context(tc.tile_pool(name="gpool", bufs=2))
-        opool = ctx.enter_context(tc.tile_pool(name="opool", bufs=8))
+        opool = ctx.enter_context(tc.tile_pool(name="opool", bufs=4))
         ps = ctx.enter_context(tc.psum_pool(name="ps", bufs=1))
         ctx.enter_context(tc.manual_schedule())
 
@@ -45,8 +45,8 @@ def tile_mex_t_kernel(tc, x, offsets, out):
         nmb = keep.tile([P, 8], F32)
         mbc = keep.tile([P, 8], F32)
         ebp = keep.tile([P, 8, 1024], BF16)
-        ebc = keep.tile([P, 2, 1024], U32, align_bytes=64)
-        ebs = keep.tile([P, 2, 1024], U8, align_bytes=64)
+        ebc = keep.tile([P, 4, 2, 256], U32, align_bytes=64)
+        ebs = keep.tile([P, 4, 2, 256], U8, align_bytes=64)
         xq = keep.tile([P, 2, 1232], BF16)
         t0 = keep.tile([P, 2, 666], BF16)
         t1 = keep.tile([P, 2, 666], BF16)
@@ -274,12 +274,11 @@ def tile_mex_t_kernel(tc, x, offsets, out):
             )
 
         def quantise_eb(mp, ebg):
-            for g in range(2):
-                nc.vector.quantize_mx(
-                    out=ebc[:, g, mp * 256 : (mp + 1) * 256].bitcast(FP8X4),
-                    scales=ebs[:, g, mp * 256 : (mp + 1) * 256],
-                    in_=ebg[:, g].rearrange("p m v -> p (m v)").bitcast(BF16),
-                )
+            nc.vector.quantize_mx(
+                out=ebc[:, mp].rearrange("p g n -> p (g n)").bitcast(FP8X4),
+                scales=ebs[:, mp].rearrange("p g n -> p (g n)"),
+                in_=ebg[:].rearrange("p g m v -> p (g m v)").bitcast(BF16),
+            )
 
         nc.vector.memset(mt_col[:], 0.0)
         nc.scalar.activation(out=warm[:], in_=mt_col[:, 0, 0:1], func=ACT.Exp)
@@ -392,8 +391,8 @@ def tile_mex_t_kernel(tc, x, offsets, out):
             for g in range(2):
                 nc.tensor.matmul_mx(
                     out=acc[:],
-                    lhsT=ebc[:, g, mt * P : (mt + 1) * P].bitcast(FP8X4),
-                    lhsT_scale=ebs[:, g, mt * P : (mt + 1) * P],
+                    lhsT=ebc[:, mt // 2, g, (mt % 2) * P : (mt % 2 + 1) * P].bitcast(FP8X4),
+                    lhsT_scale=ebs[:, mt // 2, g, (mt % 2) * P : (mt % 2 + 1) * P],
                     rhs=exc[:, 2 * i + hh, g, :].bitcast(FP8X4),
                     rhs_scale=exs[:, 2 * i + hh, g, :],
                     start=(g == 0),
@@ -412,6 +411,9 @@ def tile_mex_t_kernel(tc, x, offsets, out):
         pool_step(4, 1)
         unit_add_class1(dps0, 0, 0)
         eb_of_unit = {2: (0,), 3: (1,), 4: (2, 3), 5: (4,), 6: (5, 6), 7: (7,)}
+        nc.vector.tensor_scalar(
+            out=mbc[:], in0=nmb[:], scalar1=-1.0, scalar2=-math.log(1024.0), op0=ALU.mult, op1=ALU.add
+        )
         for u in range(8):
             hh, i = units[u]
             e_tiles[u] = epool.tile([P, 2, 2048], BF16, name="et_ex", align_bytes=64)
@@ -461,32 +463,33 @@ def tile_mex_t_kernel(tc, x, offsets, out):
             for mt in eb_of_unit.get(u, ()):
                 eb_codes(mt)
             quantise_ex(hh, i, e_tiles[u])
-        nc.vector.tensor_scalar(
-            out=mbc[:], in0=nmb[:], scalar1=-1.0, scalar2=-math.log(1024.0), op0=ALU.mult, op1=ALU.add
-        )
-
-        for i in range(4):
-            for mt in range(8):
-                ot = opool.tile([P, 1024], F32, name="ot")
-                last = (i == 3 and mt == 7) or (i == 0 and mt == 0)
-                for hh in range(2):
+        pieces_of_tile = {**{t: (16, 16) for t in range(4)}, 31: (16, 16)}
+        for t in range(32):
+            i, mt = divmod(t, 8)
+            if t % 2 == 0:
+                ot = opool.tile([P, 2, 1024], F32, name="ot")
+            o = ot[:, t % 2, :]
+            pair = 40 <= t < 40
+            row = 0
+            for n, rows in enumerate(pieces_of_tile.get(t, (32,))):
+                todo = rows
+                while todo:
+                    hh, r0 = divmod(row, 16)
+                    nr = min(todo, 16 - r0)
                     if (i, mt, hh) not in sums:
                         mx_group(i, mt, hh)
-                    acc = sums[(i, mt, hh)]
                     nc.scalar.activation(
-                        out=ot[:, hh * 512 : (hh + 1) * 512].rearrange("p (hl a bb) -> p hl a bb", a=8, bb=4),
-                        in_=acc[:].rearrange("p (bb hl a) -> p hl a bb", bb=4, a=8),
+                        out=o[:, 32 * row : 32 * (row + nr)].rearrange("p (hl a bb) -> p hl a bb", a=8, bb=4),
+                        in_=sums[(i, mt, hh)][:].rearrange("p (bb hl a) -> p hl a bb", bb=4, a=8)[:, r0 : r0 + nr],
                         func=ACT.Ln,
                     )
-                    if last:
-                        s = slice(hh * 512, (hh + 1) * 512)
-                        nc.vector.scalar_tensor_tensor(
-                            out=ot[:, s], in0=ot[:, s], scalar=mbc[:, mt : mt + 1], in1=mxs[:, i, s],
-                            op0=ALU.add, op1=ALU.add,
-                        )
-                        nc.sync.dma_start(out=ov[i][:, mt, s], in_=ot[:, s])
-                if not last:
-                    nc.vector.scalar_tensor_tensor(
-                        out=ot[:], in0=ot[:], scalar=mbc[:, mt : mt + 1], in1=mxs[:, i, :], op0=ALU.add, op1=ALU.add
-                    )
-                    nc.sync.dma_start(out=ov[i][:, mt, :], in_=ot[:])
+                    row += nr
+                    todo -= nr
+                s = slice(32 * (row - rows), 32 * row)
+                nc.vector.scalar_tensor_tensor(
+                    out=o[:, s], in0=o[:, s], scalar=mbc[:, mt : mt + 1], in1=mxs[:, i, s], op0=ALU.add, op1=ALU.add
+                )
+                if not pair:
+                    nc.sync.dma_start(out=ov[i][:, mt, s], in_=o[:, s])
+            if pair and t % 2 == 1:
+                nc.sync.dma_start(out=ov[i][:, mt - 1 : mt + 1, :], in_=ot[:])

@@ -363,7 +363,7 @@ def tile_mex_t_kernel(tc, x, offsets, out):
         def prepare_g(u):
             hh, i = units[u]
             d_tiles[u] = dpool.tile([P, 2, 2, 512], F32, name="dt")
-            if u not in (1, 3, 5, 7):
+            if u not in (1, 3, 7):
                 for g in range(2):
                     for q in range(2):
                         subtract_part(nc.gpsimd, mx_sbuf(u), i, hh, 3, d_tiles[u], g, q)
@@ -371,7 +371,7 @@ def tile_mex_t_kernel(tc, x, offsets, out):
         def prepare_v(u):
             hh, i = units[u]
             subtract(nc.vector, mx_psum(u), i, hh, 2, d_tiles[u][:, 0])
-            if u in (1, 3, 5, 7):
+            if u in (1, 3, 7):
                 subtract(nc.vector, mx_psum(u), i, hh, 3, d_tiles[u][:, 1])
 
         def eb_codes(mt):

@@ -25,7 +25,7 @@ def tile_mex_t_kernel(tc, x, offsets, out):
         dpool = ctx.enter_context(tc.tile_pool(name="dpool", bufs=4))
         epool = ctx.enter_context(tc.tile_pool(name="epool", bufs=3))
         gpool = ctx.enter_context(tc.tile_pool(name="gpool", bufs=2))
-        opool = ctx.enter_context(tc.tile_pool(name="opool", bufs=4))
+        opool = ctx.enter_context(tc.tile_pool(name="opool", bufs=8))
         ps = ctx.enter_context(tc.psum_pool(name="ps", bufs=1))
         ctx.enter_context(tc.manual_schedule())
 
@@ -463,33 +463,24 @@ def tile_mex_t_kernel(tc, x, offsets, out):
             for mt in eb_of_unit.get(u, ()):
                 eb_codes(mt)
             quantise_ex(hh, i, e_tiles[u])
-        pieces_of_tile = {**{t: (16, 16) for t in range(4)}, 31: (16, 16)}
-        for t in range(32):
-            i, mt = divmod(t, 8)
-            if t % 2 == 0:
-                ot = opool.tile([P, 2, 1024], F32, name="ot")
-            o = ot[:, t % 2, :]
-            pair = 40 <= t < 40
-            row = 0
-            for n, rows in enumerate(pieces_of_tile.get(t, (32,))):
-                todo = rows
-                while todo:
-                    hh, r0 = divmod(row, 16)
-                    nr = min(todo, 16 - r0)
+        for i in range(4):
+            for mt in range(8):
+                ot = opool.tile([P, 1024], F32, name="ot")
+                in_halves = (i == 0 and mt < 4) or (i == 3 and mt == 7)
+                for hh in range(2):
                     if (i, mt, hh) not in sums:
                         mx_group(i, mt, hh)
+                    s = slice(hh * 512, (hh + 1) * 512)
                     nc.scalar.activation(
-                        out=o[:, 32 * row : 32 * (row + nr)].rearrange("p (hl a bb) -> p hl a bb", a=8, bb=4),
-                        in_=sums[(i, mt, hh)][:].rearrange("p (bb hl a) -> p hl a bb", bb=4, a=8)[:, r0 : r0 + nr],
+                        out=ot[:, s].rearrange("p (hl a bb) -> p hl a bb", a=8, bb=4),
+                        in_=sums[(i, mt, hh)][:].rearrange("p (bb hl a) -> p hl a bb", bb=4, a=8),
                         func=ACT.Ln,
                     )
-                    row += nr
-                    todo -= nr
-                s = slice(32 * (row - rows), 32 * row)
-                nc.vector.scalar_tensor_tensor(
-                    out=o[:, s], in0=o[:, s], scalar=mbc[:, mt : mt + 1], in1=mxs[:, i, s], op0=ALU.add, op1=ALU.add
-                )
-                if not pair:
-                    nc.sync.dma_start(out=ov[i][:, mt, s], in_=o[:, s])
-            if pair and t % 2 == 1:
-                nc.sync.dma_start(out=ov[i][:, mt - 1 : mt + 1, :], in_=ot[:])
+                    nc.vector.scalar_tensor_tensor(
+                        out=ot[:, s], in0=ot[:, s], scalar=mbc[:, mt : mt + 1], in1=mxs[:, i, s],
+                        op0=ALU.add, op1=ALU.add,
+                    )
+                    if in_halves:
+                        nc.sync.dma_start(out=ov[i][:, mt, s], in_=ot[:, s])
+                if not in_halves:
+                    nc.sync.dma_start(out=ov[i][:, mt, :], in_=ot[:])

import math
from contextlib import ExitStack

import concourse.mybir as mybir
from concourse.masks import make_identity

FLOPS = 2 * 1024 * 1024 * 4096

BF16 = mybir.dt.bfloat16
F32 = mybir.dt.float32
U32 = mybir.dt.uint32
U8 = mybir.dt.uint8
FP8X4 = mybir.dt.float8_e4m3fn_x4
ALU = mybir.AluOpType
ACT = mybir.ActivationFunctionType
AX = mybir.AxisListType

P = 128


def tile_mex_t_kernel(tc, x, offsets, out):
    nc = tc.nc
    with ExitStack() as ctx:
        keep = ctx.enter_context(tc.tile_pool(name="keep", bufs=1))
        dpool = ctx.enter_context(tc.tile_pool(name="dpool", bufs=4))
        epool = ctx.enter_context(tc.tile_pool(name="epool", bufs=3))
        gpool = ctx.enter_context(tc.tile_pool(name="gpool", bufs=2))
        opool = ctx.enter_context(tc.tile_pool(name="opool", bufs=8))
        ps = ctx.enter_context(tc.psum_pool(name="ps", bufs=1))
        ctx.enter_context(tc.manual_schedule())

        xq_v = x.rearrange("i (ch cl) h w -> (i ch) cl (h w)", cl=2)
        bv = offsets.rearrange("o (p mt) c h w -> p (o mt) (c h w)", mt=8)
        ov = out.rearrange("i (p mt) h w -> i p mt (h w)", mt=8)

        ident = keep.tile([P, P], BF16)
        ident32 = keep.tile([P, P], F32)
        nsel = keep.tile([P, 4, P], BF16)
        negr = keep.tile([P, P, 4], BF16)
        b_sb = keep.tile([P, 8, 1024], BF16)
        tr1 = keep.tile([P, 4, 512], BF16)
        tr2 = keep.tile([P, 4, 256], BF16)
        tr3 = keep.tile([P, 4, 128], BF16)
        warm = keep.tile([P, 1], F32)
        nmb = keep.tile([P, 8], F32)
        mbc = keep.tile([P, 8], F32)
        ebp = keep.tile([P, 8, 1024], BF16)
        ebc = keep.tile([P, 4, 2, 256], U32, align_bytes=64)
        ebs = keep.tile([P, 4, 2, 256], U8, align_bytes=64)
        xq = keep.tile([P, 2, 1232], BF16)
        t0 = keep.tile([P, 2, 666], BF16)
        t1 = keep.tile([P, 2, 666], BF16)
        t2 = keep.tile([P, 2, 666], BF16)
        t3 = keep.tile([P, 2, 666], BF16)
        p4 = keep.tile([P, 2, 512], BF16)
        mt_col = keep.tile([P, 2, 32], BF16)
        negm = keep.tile([P, 2, 4, 32], F32)
        mxs = keep.tile([P, 4, 1024], BF16)
        xs01 = keep.tile([P, 2, 2, 1120], BF16)
        xs23 = keep.tile([P, 2, 2, 1120], BF16)
        xs = [xs01, xs23]
        exc = keep.tile([P, 8, 2, 512], U32, align_bytes=64)
        exs = keep.tile([P, 8, 2, 512], U8, align_bytes=64)
        CHUNK_BANKS = 4
        SIDE_BANKS = (4, 5)
        side_no = [0]
        MX_BANK = 6
        mxp = [None, None]

        def bank(k, shape, dtype):
            return ps.tile(shape, dtype, tag="bank%d" % k, name="bk%d" % k)

        def side_bank(shape, dtype):
            side_no[0] += 1
            return bank(SIDE_BANKS[side_no[0] % 2], shape, dtype)

        def load_x_rows(pr):
            rows = x[2 * pr : 2 * pr + 2].rearrange("i (g c) h w -> c (i g) (h w)", g=2)
            for dh in range(4):
                nc.sync.dma_start(
                    out=xs[pr][dh:P:4].rearrange("p i g n -> p (i g) n"),
                    in_=rows[:, :, 35 * dh : 35 * dh + 1120],
                )

        def max_step(level, m0, n, s0):
            s = slice(m0, m0 + n)
            q = slice(s0, s0 + n)
            if level == 1:
                nc.vector.tensor_max(out=tr1[:, q, :], in0=b_sb[:, s, 0:512], in1=b_sb[:, s, 512:1024])
            elif level == 2:
                nc.vector.tensor_max(out=tr2[:, q, :], in0=tr1[:, q, 0:256], in1=tr1[:, q, 256:512])
            else:
                nc.vector.tensor_reduce(out=nmb[:, s], in_=tr2[:, q, :], axis=AX.X, op=ALU.max, negate=True)

        def exp_of_b(mt):
            nc.scalar.activation(
                out=ebp[:, mt, :],
                in_=b_sb[:, mt, :],
                func=ACT.Exp,
                bias=nmb[:, mt : mt + 1],
                scale=1.0,
            )

        def pool_step(step, hh):
            f0 = 560 * hh
            if step == 1:
                nc.vector.tensor_max(out=t0[:, hh, 0:665], in0=xq[:, 0, f0 : f0 + 665], in1=xq[:, 1, f0 : f0 + 665])
            elif step == 2:
                nc.vector.tensor_max(out=t1[:, hh, 0:664], in0=t0[:, hh, 0:664], in1=t0[:, hh, 1:665])
            elif step == 3:
                nc.vector.tensor_max(out=t2[:, hh, 0:662], in0=t1[:, hh, 0:662], in1=t1[:, hh, 2:664])
            elif step == 4:
                nc.vector.tensor_max(out=t3[:, hh, 0:627], in0=t2[:, hh, 0:627], in1=t2[:, hh, 35:662])
            else:
                nc.vector.tensor_max(
                    out=p4[:, hh, :].rearrange("p (h w) -> p h w", w=32),
                    in0=t3[:, hh, 0:560].rearrange("p (h w) -> p h w", w=35)[:, :, 0:32],
                    in1=t3[:, hh, 70:630].rearrange("p (h w) -> p h w", w=35)[:, :, 0:32],
                )

        def transpose_pooled(hh):
            pt = side_bank([P, 5, P], BF16)
            for jj in range(4):
                nc.tensor.transpose(pt[:, jj, :], p4[:, hh, jj * P : (jj + 1) * P], ident[:])
            nc.tensor.transpose(pt[:, 4, :], p4[:, hh, :].rearrange("p (q bb) -> p q bb", bb=4)[:, :, 0], ident[:])
            return pt

        def max_over_channels(hh, pt):
            with nc.allow_low_precision(reason="a maximum of bfloat16 values is a bfloat16 value"):
                nc.vector.tensor_reduce(
                    out=mt_col[:, hh, 0:20],
                    in_=pt[:].rearrange("p j (i c) -> p (j i) c", c=32),
                    axis=AX.X,
                    op=ALU.max,
                )

        def select_negated(hh):
            selp = side_bank([P, 4, 32], F32)
            for b in range(4):
                nc.tensor.matmul(out=selp[:, b, :], lhsT=nsel[:, b, :], rhs=mt_col[:, hh, :], start=True, stop=True)
            return selp

        def copy_negated(hh, selp):
            nc.vector.tensor_copy(out=negm[:, hh], in_=selp[:])

        def spread_mx(hh, pr, ils=(0, 1)):
            if 0 in ils:
                mxp[pr] = bank(MX_BANK + pr, [P, 2, 512], BF16)
            for il in ils:
                for jj in range(4):
                    k = 4 * jj + 2 * pr + il
                    nc.tensor.transpose(
                        mxp[pr][:, il, jj * P : (jj + 1) * P], mt_col[:, hh, k : k + 1].to_broadcast([P, P]), ident[:]
                    )

        def copy_mx(hh, pr):
            nc.vector.tensor_copy(out=mxs[:, 2 * pr : 2 * pr + 2, hh * 512 : (hh + 1) * 512], in_=mxp[pr][:])

        chunk_no = [0]

        def unit_banks():
            dps = {}
            for b in range(2):
                for g in range(2):
                    dps[(g, b)] = bank(chunk_no[0] % CHUNK_BANKS, [P, 512], F32)
                    chunk_no[0] += 1
            return dps

        def copy_x(dps, g, b, i, hh):
            rows = xs[i // 2][:, i % 2, g, :].rearrange("p (h w) -> p h w", w=35)
            nc.tensor.matmul(
                out=dps[(g, b)][:].rearrange("p (r w) -> p r w", w=32),
                lhsT=ident[:],
                rhs=rows[:, 16 * hh : 16 * hh + 16, b : b + 32],
                start=True,
                stop=False,
            )

        def add_class0(dps, g, i, hh):
            nc.tensor.matmul(
                out=dps[(g, 0)][:],
                lhsT=mt_col[:, hh, 16 + i : 17 + i].to_broadcast([P, P]),
                rhs=negr[:].rearrange("p q d -> p (q d)"),
                start=False,
                stop=True,
            )

        def unit_add_class1(dps, i, hh):
            for g in range(2):
                for jj in range(4):
                    k = 4 * jj + i
                    nc.tensor.matmul(
                        out=dps[(g, 1)][:, jj * P : (jj + 1) * P],
                        lhsT=negm[:, hh, 1, k : k + 1].to_broadcast([P, P]),
                        rhs=ident32[:],
                        is_transpose=True,
                        start=False,
                        stop=(jj == 3),
                    )

        def unit_on_pe(i, hh, between=None):
            dps = unit_banks()
            for g in range(2):
                copy_x(dps, g, 0, i, hh)
                add_class0(dps, g, i, hh)
            if between:
                between()
            for g in range(2):
                copy_x(dps, g, 1, i, hh)
            unit_add_class1(dps, i, hh)
            return dps

        def exp_chunks(dps, b, e_tile):
            for g in range(2):
                nc.scalar.activation(out=e_tile[:, g, b * 512 : (b + 1) * 512], in_=dps[(g, b)][:], func=ACT.Exp)

        def subtract(eng, m_ap, i, hh, b, d_view):
            eng.tensor_tensor(
                out=d_view.rearrange("p g (hl a d) -> p g hl a d", a=8, d=4),
                in0=xs[i // 2][:, i % 2, :, :]
                .rearrange("p g (h w) -> p g h w", w=35)[:, :, 16 * hh : 16 * hh + 16, b : b + 32]
                .rearrange("p g hl (a d) -> p g hl a d", d=4),
                in1=m_ap
                .rearrange("p (hl a bb) -> p hl a bb", a=8, bb=4)[:, :, :, b]
                .unsqueeze(1)
                .unsqueeze(4)
                .to_broadcast([P, 2, 16, 8, 4]),
                op=ALU.subtract,
            )

        def subtract_part(eng, m_ap, i, hh, b, d_tile, g, q):
            h0 = 16 * hh + 8 * q
            eng.tensor_tensor(
                out=d_tile[:, b - 2, g, 256 * q : 256 * q + 256].rearrange("p (hl a d) -> p hl a d", a=8, d=4),
                in0=xs[i // 2][:, i % 2, g, :]
                .rearrange("p (h w) -> p h w", w=35)[:, h0 : h0 + 8, b : b + 32]
                .rearrange("p hl (a d) -> p hl a d", d=4),
                in1=m_ap[:, 256 * q : 256 * q + 256]
                .rearrange("p (hl a bb) -> p hl a bb", a=8, bb=4)[:, :, :, b]
                .unsqueeze(3)
                .to_broadcast([P, 8, 8, 4]),
                op=ALU.subtract,
            )

        def exp_piece(d_tile, e_tile):
            nc.scalar.activation(
                out=e_tile[:, :, 1024:2048].rearrange("p g (b n) -> p g b n", b=2),
                in_=d_tile[:].rearrange("p b g n -> p g b n"),
                func=ACT.Exp,
            )

        def exp_class(b, d_tile, e_tile):
            nc.scalar.activation(out=e_tile[:, :, b * 512 : (b + 1) * 512], in_=d_tile[:, b - 2], func=ACT.Exp)

        def quantise_ex(hh, i, e_tile):
            nc.vector.quantize_mx(
                out=exc[:, 2 * i + hh].rearrange("p g n -> p (g n)").bitcast(FP8X4),
                scales=exs[:, 2 * i + hh].rearrange("p g n -> p (g n)"),
                in_=e_tile[:].rearrange("p g n -> p (g n)"),
            )

        def transpose_eb(mt):
            et = side_bank([P, 4, P], F32)
            words = ebp[:, mt, :].bitcast(F32)
            for g in range(2):
                for v in range(2):
                    nc.tensor.transpose(et[:, 2 * g + v, :], words[:, 256 * g + v : 256 * (g + 1) : 2], ident32[:])
            return et

        def regroup_eb(mt, et, ebg):
            ml = mt % 2
            nc.vector.tensor_copy(
                out=ebg[:, :, ml * P : (ml + 1) * P, :], in_=et[:].rearrange("p (g v) m -> p g m v", g=2)
            )

        def quantise_eb(mp, ebg):
            nc.vector.quantize_mx(
                out=ebc[:, mp].rearrange("p g n -> p (g n)").bitcast(FP8X4),
                scales=ebs[:, mp].rearrange("p g n -> p (g n)"),
                in_=ebg[:].rearrange("p g m v -> p (g m v)").bitcast(BF16),
            )

        nc.vector.memset(mt_col[:], 0.0)
        nc.scalar.activation(out=warm[:], in_=mt_col[:, 0, 0:1], func=ACT.Exp)
        make_identity(nc, ident[:])
        nc.vector.tensor_copy(out=ident32[:], in_=ident[:])
        nc.vector.tensor_scalar_mul(out=negr[:], in0=ident[:].unsqueeze(2).to_broadcast([P, P, 4]), scalar1=-1.0)
        for b in range(4):
            nc.vector.tensor_scalar_mul(
                out=nsel[:, b, :].rearrange("p (r a d) -> p r a d", a=8, d=4),
                in0=ident[:]
                .rearrange("p (r a bb) -> p r a bb", a=8, bb=4)[:, :, :, b]
                .unsqueeze(3)
                .to_broadcast([P, 4, 8, 4]),
                scalar1=-1.0,
            )

        nc.sync.dma_start(out=b_sb[:, 0:1, :], in_=bv[:, 0:1, :])
        nc.sync.dma_start(out=b_sb[:, 1:2, :], in_=bv[:, 1:2, :])
        nc.sync.dma_start(out=b_sb[:, 2:4, :], in_=bv[:, 2:4, :])
        nc.sync.dma_start(out=xq[:, :, 0:672], in_=xq_v[:, :, 0:672])
        nc.sync.dma_start(out=b_sb[:, 4:6, :], in_=bv[:, 4:6, :])
        load_x_rows(0)
        nc.sync.dma_start(out=xq[:, :, 672:1225], in_=xq_v[:, :, 672:1225])
        nc.sync.dma_start(out=b_sb[:, 6:8, :], in_=bv[:, 6:8, :])
        load_x_rows(1)

        max_step(1, 0, 1, 0)
        max_step(2, 0, 1, 0)
        max_step(1, 1, 1, 1)
        max_step(3, 0, 1, 0)
        exp_of_b(0)
        max_step(2, 1, 1, 1)
        max_step(1, 2, 1, 2)
        max_step(3, 1, 1, 1)
        exp_of_b(1)
        pool_step(1, 0)
        max_step(2, 2, 1, 2)
        max_step(1, 3, 1, 3)
        pool_step(2, 0)
        max_step(3, 2, 1, 2)
        exp_of_b(2)
        pool_step(3, 0)
        max_step(2, 3, 1, 3)
        max_step(1, 4, 1, 0)
        pool_step(4, 0)
        max_step(3, 3, 1, 3)
        exp_of_b(3)
        pool_step(5, 0)
        pt0 = transpose_pooled(0)
        dps0 = unit_banks()
        for g in range(2):
            copy_x(dps0, g, 0, 0, 0)
        max_step(2, 4, 1, 0)
        max_step(1, 5, 1, 1)
        max_step(3, 4, 1, 0)
        exp_of_b(4)
        max_step(2, 5, 1, 1)
        max_over_channels(0, pt0)
        spread_mx(0, 0, (0,))
        for g in range(2):
            add_class0(dps0, g, 0, 0)
        sp0 = select_negated(0)
        for g in range(2):
            copy_x(dps0, g, 1, 0, 0)
        max_step(3, 5, 1, 1)
        exp_of_b(5)
        pool_step(1, 1)

        units = [(hh, i) for hh in range(2) for i in range(4)]
        d_tiles = {}
        e_tiles = {}
        ebg_now = [None]

        def mx_sbuf(u):
            hh, i = units[u]
            return mxs[:, i, hh * 512 : (hh + 1) * 512]

        def mx_psum(u):
            hh, i = units[u]
            return mxp[i // 2][:, i % 2, :]

        def prepare_g(u):
            hh, i = units[u]
            d_tiles[u] = dpool.tile([P, 2, 2, 512], F32, name="dt")
            if u not in (1, 3, 7):
                for g in range(2):
                    for q in range(2):
                        subtract_part(nc.gpsimd, mx_sbuf(u), i, hh, 3, d_tiles[u], g, q)

        def prepare_v(u):
            hh, i = units[u]
            subtract(nc.vector, mx_psum(u), i, hh, 2, d_tiles[u][:, 0])
            if u in (1, 3, 7):
                subtract(nc.vector, mx_psum(u), i, hh, 3, d_tiles[u][:, 1])

        def eb_codes(mt):
            et = transpose_eb(mt)
            if mt % 2 == 0:
                ebg_now[0] = gpool.tile([P, 2, 256, 2], F32, name="ebg", align_bytes=64)
            regroup_eb(mt, et, ebg_now[0])
            if mt % 2 == 1:
                quantise_eb(mt // 2, ebg_now[0])

        ACC_ORDER = [6, 7, 5, 4, 0, 1, 2, 3]
        sums = {}

        def mx_group(i, mt, hh):
            acc = bank(ACC_ORDER[len(sums) % 8], [P, 512], F32)
            sums[(i, mt, hh)] = acc
            for g in range(2):
                nc.tensor.matmul_mx(
                    out=acc[:],
                    lhsT=ebc[:, mt // 2, g, (mt % 2) * P : (mt % 2 + 1) * P].bitcast(FP8X4),
                    lhsT_scale=ebs[:, mt // 2, g, (mt % 2) * P : (mt % 2 + 1) * P],
                    rhs=exc[:, 2 * i + hh, g, :].bitcast(FP8X4),
                    rhs_scale=exs[:, 2 * i + hh, g, :],
                    start=(g == 0),
                    stop=(g == 1),
                )

        d_tiles[0] = dpool.tile([P, 2, 2, 512], F32, name="dt")
        subtract(nc.vector, mx_psum(0), 0, 0, 2, d_tiles[0][:, 0])
        pool_step(2, 1)
        copy_negated(0, sp0)
        max_step(1, 6, 2, 2)
        subtract(nc.vector, mx_psum(0), 0, 0, 3, d_tiles[0][:, 1])
        max_step(2, 6, 2, 2)
        pool_step(3, 1)
        max_step(3, 6, 2, 2)
        pool_step(4, 1)
        unit_add_class1(dps0, 0, 0)
        eb_of_unit = {2: (0,), 3: (1,), 4: (2, 3), 5: (4,), 6: (5, 6), 7: (7,)}
        nc.vector.tensor_scalar(
            out=mbc[:], in0=nmb[:], scalar1=-1.0, scalar2=-math.log(1024.0), op0=ALU.mult, op1=ALU.add
        )
        for u in range(8):
            hh, i = units[u]
            e_tiles[u] = epool.tile([P, 2, 2048], BF16, name="et_ex", align_bytes=64)
            if u == 0:
                dps = dps0
            elif u == 1:
                dps = unit_on_pe(i, hh, lambda: spread_mx(0, 1))
            else:
                dps = unit_on_pe(i, hh)
            exp_chunks(dps, 0, e_tiles[u])
            if u == 0:
                exp_class(2, d_tiles[u], e_tiles[u])
                exp_chunks(dps, 1, e_tiles[u])
                exp_class(3, d_tiles[u], e_tiles[u])
                exp_of_b(6)
                exp_of_b(7)
                spread_mx(0, 0, (1,))
                pool_step(5, 1)
                copy_mx(0, 0)
                prepare_g(1)
                prepare_v(1)
            else:
                if u == 1:
                    copy_mx(0, 1)
                    prepare_g(2)
                    prepare_g(3)
                exp_chunks(dps, 1, e_tiles[u])
                exp_piece(d_tiles[u], e_tiles[u])
            if u == 1:
                prepare_v(2)
                pt1 = transpose_pooled(1)
                max_over_channels(1, pt1)
                prepare_v(3)
            if u == 3:
                sp1 = select_negated(1)
                copy_negated(1, sp1)
            if u == 2 or u == 3:
                spread_mx(1, u - 2)
                copy_mx(1, u - 2)
            if 2 <= u < 6:
                prepare_g(u + 2)
            if 3 <= u < 7:
                prepare_v(u + 1)
            if u == 7:
                for early in ((0, 0, 0), (0, 0, 1), (0, 1, 0)):
                    mx_group(*early)
            for mt in eb_of_unit.get(u, ()):
                eb_codes(mt)
            quantise_ex(hh, i, e_tiles[u])
        for i in range(4):
            for mt in range(8):
                ot = opool.tile([P, 1024], F32, name="ot")
                in_halves = (i == 0 and mt < 4) or (i == 3 and mt == 7)
                for hh in range(2):
                    if (i, mt, hh) not in sums:
                        mx_group(i, mt, hh)
                    s = slice(hh * 512, (hh + 1) * 512)
                    nc.scalar.activation(
                        out=ot[:, s].rearrange("p (hl a bb) -> p hl a bb", a=8, bb=4),
                        in_=sums[(i, mt, hh)][:].rearrange("p (bb hl a) -> p hl a bb", bb=4, a=8),
                        func=ACT.Ln,
                    )
                    nc.vector.scalar_tensor_tensor(
                        out=ot[:, s], in0=ot[:, s], scalar=mbc[:, mt : mt + 1], in1=mxs[:, i, s],
                        op0=ALU.add, op1=ALU.add,
                    )
                    if in_halves:
                        nc.sync.dma_start(out=ov[i][:, mt, s], in_=ot[:, s])
                if not in_halves:
                    nc.sync.dma_start(out=ov[i][:, mt, :], in_=ot[:])
